import numpy as np
import ml_dtypes


def mxq(x, axis, fmt="e4m3"):
    dtype, down = {"e4m3": (ml_dtypes.float8_e4m3fn, 7), "e5m2": (ml_dtypes.float8_e5m2, 14)}[fmt]
    v = np.moveaxis(np.asarray(x, np.float32).astype(ml_dtypes.bfloat16).astype(np.float64), axis, -1)
    blocks = v.reshape(v.shape[:-1] + (-1, 32))
    amax = np.abs(blocks).max(-1, keepdims=True)
    byte = np.maximum(np.where(amax > 0, np.frexp(amax)[1] - 1 + 127, 0) - down, 1)
    scale = np.exp2(byte - 127.0)
    codes = (blocks / scale).astype(np.float32).astype(dtype).astype(np.float64)
    return np.moveaxis((codes * scale).reshape(v.shape), -1, axis)


WIDE = False


def mx_kscale(k):
    if not WIDE:
        return np.ones(k)
    levels = np.array([10, -10, 5, -5, 0])
    a = np.random.permutation(np.resize(levels, k // 512 * 4)).reshape(k // 512, 4)
    idx = np.arange(k)
    return np.exp2(a[idx // 512, idx % 128 // 32])


BF16 = ml_dtypes.bfloat16


def bf(x):
    return np.asarray(x, np.float32).astype(BF16)


def f64(x):
    return np.asarray(x).astype(np.float64)


B, IN, OUT = 512, 1024, 1024
G = 3 * OUT


def sigmoid(v):
    return 1.0 / (1.0 + np.exp(-v))


def setup_inputs():
    s = mx_kscale(OUT)
    return {
        "xg": bf(np.random.standard_normal((B, G)) * 0.75),
        "hx": bf(np.random.standard_normal((B, OUT)) * s),
        "cx": bf(np.random.standard_normal((B, OUT))),
        "td0": bf(np.random.uniform(0.0, 1.0, B)),
        "td1": bf(np.random.uniform(0.0, 1.0, B)),
        "w_hh": bf(np.random.standard_normal((G, OUT)) * 0.7 / np.sqrt(OUT) / s),
        "w_pi": bf(np.random.standard_normal((OUT, OUT)) * 0.7 / np.sqrt(OUT)),
        "w_pf": bf(np.random.standard_normal((OUT, OUT)) * 0.7 / np.sqrt(OUT)),
        "b_hh": bf(np.random.standard_normal(G) * 0.3),
        "a": bf(1.0 + 0.1 * np.random.standard_normal(1)),
        "b": bf(0.5 + 0.1 * np.random.standard_normal(1)),
    }


def reference(xg, hx, cx, td0, td1, w_hh, w_pi, w_pf, b_hh, a, b):
    c = f64(cx)
    cq = mxq(c, 1, "e4m3")
    gates = f64(xg) + (mxq(f64(hx), 1, "e4m3") @ mxq(f64(w_hh), 1, "e4m3").T) + f64(b_hh)
    i_g, f_g, g_g = np.split(gates, 3, axis=1)
    i_g = sigmoid(i_g + (cq @ mxq(f64(w_pi), 1, "e4m3").T))
    f_g = sigmoid(f_g + (cq @ mxq(f64(w_pf), 1, "e4m3").T))
    g_g = np.tanh(g_g)
    forcoff = (f64(a) * np.exp(-f64(b) * f64(td0)))[:, None]
    incoff = (f64(a) * np.exp(-f64(b) * f64(td1)))[:, None]
    f_g = forcoff * f_g
    i_g = incoff * i_g
    return f_g * c + i_g * g_g

@@ -1,0 +1,220 @@
+from contextlib import ExitStack
+
+import concourse.mybir as mybir
+from concourse.masks import make_identity
+
+F32 = mybir.dt.float32
+BF16 = mybir.dt.bfloat16
+U32 = mybir.dt.uint32
+U8 = mybir.dt.uint8
+FP8X4 = mybir.dt.float8_e4m3fn_x4
+ACT = mybir.ActivationFunctionType
+ALU = mybir.AluOpType
+
+P = 128
+B = 512
+K = 1024
+OUT = 1024
+GATES = ("i", "f", "g")
+K_PASS = 512
+PASSES = K // K_PASS
+BLOCK = 512
+ROW_TILES = BLOCK // P
+BATCH_TILES = B // P
+HALVES = OUT // BLOCK
+WORDS = K // 2
+
+FLOPS = 2 * B * K * (3 * OUT + 2 * OUT)
+
+
+def tile_ircnn_lstmcell_pa_kernel(
+    tc, xg, hx, cx, td0, td1, w_hh, w_pi, w_pf, b_hh, a, b, out
+):
+    nc = tc.nc
+    with ExitStack() as ctx:
+        const = ctx.enter_context(tc.tile_pool(name="const", bufs=1))
+        raw_pool = ctx.enter_context(tc.tile_pool(name="raw", bufs=7))
+        grouped_pool = ctx.enter_context(tc.tile_pool(name="grouped", bufs=3))
+        weight_pool = ctx.enter_context(tc.tile_pool(name="weight", bufs=3))
+        gate_pool = ctx.enter_context(tc.tile_pool(name="gate", bufs=1))
+        flip_psum = ctx.enter_context(tc.psum_pool(name="flip", bufs=4))
+        acc_psum = ctx.enter_context(tc.psum_pool(name="acc", bufs=4))
+
+        bias_row = const.tile([P, 3 * OUT], BF16, name="bias_row")
+        nc.vector.memset(bias_row[:], 0.0)
+        nc.scalar.dma_start(out=bias_row[0:1, :], in_=b_hh.rearrange("(o c) -> o c", o=1))
+        td_rows = const.tile([P, P], BF16, name="td_rows")
+        nc.vector.memset(td_rows[:], 0.0)
+        nc.scalar.dma_start(
+            out=td_rows[0:BATCH_TILES, :], in_=td0.rearrange("(t p) -> t p", p=P)
+        )
+        nc.scalar.dma_start(
+            out=td_rows[BATCH_TILES : 2 * BATCH_TILES, :],
+            in_=td1.rearrange("(t p) -> t p", p=P),
+        )
+        a_bf = const.tile([P, 1], BF16, name="a_bf")
+        nc.scalar.dma_start(out=a_bf[:], in_=a.partition_broadcast(P))
+        b_bf = const.tile([P, 1], BF16, name="b_bf")
+        nc.scalar.dma_start(out=b_bf[:], in_=b.partition_broadcast(P))
+
+        def load_block(rows, pool, name):
+            raw = pool.tile([P, ROW_TILES * K], BF16, name=name)
+            nc.sync.dma_start(
+                out=raw[:].rearrange("p (j k) -> p j k", j=ROW_TILES),
+                in_=rows.rearrange("(j p) k -> p j k", p=P),
+            )
+            return raw
+
+        def load_xg(gate_index, half):
+            first = gate_index * OUT + half * BLOCK
+            xg_part = gate_pool.tile(
+                [P, BATCH_TILES, BLOCK], BF16, name="xg_%s%d" % (GATES[gate_index], half)
+            )
+            nc.sync.dma_start(
+                out=xg_part[:],
+                in_=xg[:, first : first + BLOCK].rearrange("(t p) c -> p t c", p=P),
+            )
+            return xg_part
+
+        hx_raw = load_block(hx, raw_pool, "raw")
+        cx_raw = load_block(cx, const, "cx_raw")
+        peephole = {"i": w_pi, "f": w_pf}
+        blocks = []
+        xg_parts = {}
+        for half in range(HALVES):
+            for gate_index, gate in enumerate(GATES):
+                first = gate_index * OUT + half * BLOCK
+                has_peephole = gate in peephole
+                blocks.append(
+                    (half, gate_index, "hx",
+                     load_block(w_hh[first : first + BLOCK, :], raw_pool, "raw"),
+                     True, not has_peephole)
+                )
+                xg_parts[(gate_index, half)] = load_xg(gate_index, half)
+                if has_peephole:
+                    rows = peephole[gate][half * BLOCK : (half + 1) * BLOCK, :]
+                    blocks.append(
+                        (half, gate_index, "cx", load_block(rows, raw_pool, "raw"), False, True)
+                    )
+
+        ident = const.tile([P, P], F32, name="ident")
+        make_identity(nc, ident[:])
+        ones = const.tile([P, P], BF16, name="ones")
+        nc.vector.memset(ones[:], 1.0)
+
+        bias_all = const.tile([P, 3 * OUT], BF16, name="bias_all")
+        for c in range(3 * OUT // BLOCK):
+            cols = slice(c * BLOCK, (c + 1) * BLOCK)
+            spread = flip_psum.tile([P, BLOCK], F32, name="spread", tag="flip")
+            nc.tensor.matmul(out=spread[:], lhsT=ones[:], rhs=bias_row[:, cols], start=True, stop=True)
+            nc.scalar.copy(out=bias_all[:, cols], in_=spread[:])
+
+        td_rows32 = const.tile([P, P], F32, name="td_rows32")
+        nc.vector.tensor_copy(out=td_rows32[:], in_=td_rows[:])
+        td_cols = flip_psum.tile([P, P], F32, name="td_cols", tag="flip")
+        nc.tensor.transpose(td_cols[:], td_rows32[:], ident[:])
+        minus_b = const.tile([P, 1], F32, name="minus_b")
+        nc.vector.tensor_scalar_mul(out=minus_b[:], in0=b_bf[:], scalar1=-1.0)
+        a_f32 = const.tile([P, 1], F32, name="a_f32")
+        nc.vector.tensor_copy(out=a_f32[:], in_=a_bf[:])
+        decay = const.tile([P, 2 * BATCH_TILES], F32, name="decay")
+        nc.scalar.activation(
+            out=decay[:], in_=td_cols[:, 0 : 2 * BATCH_TILES], func=ACT.Exp, scale=minus_b[:, 0:1]
+        )
+        nc.vector.tensor_scalar_mul(out=decay[:], in0=decay[:], scalar1=a_f32[:, 0:1])
+
+        def quantise_block(raw, pool, name):
+            words = raw[:].bitcast(F32)
+            grouped = grouped_pool.tile([P, PASSES * BLOCK * 4], BF16, name="grouped", align_bytes=64)
+            grouped_words = grouped[:].bitcast(F32).rearrange(
+                "p (g r u) -> p g r u", g=PASSES, u=2
+            )
+            for j in range(ROW_TILES):
+                flipped = flip_psum.tile([P, 2 * PASSES, P], F32, name="flipped", tag="flip")
+                for q in range(2 * PASSES):
+                    first = j * WORDS + q * P
+                    nc.tensor.transpose(flipped[:, q, :], words[:, first : first + P], ident[:])
+                nc.scalar.copy(
+                    out=grouped_words[:, :, j * P : (j + 1) * P, :],
+                    in_=flipped[:].rearrange("p (g u) r -> p g r u", u=2),
+                )
+            codes = pool.tile([P, PASSES, BLOCK], U32, name=name + "_codes", align_bytes=64)
+            scales = pool.tile([P, PASSES, BLOCK], U8, name=name + "_scales", align_bytes=64)
+            nc.vector.quantize_mx(
+                out=codes[:].rearrange("p g r -> p (g r)").bitcast(FP8X4),
+                scales=scales[:].rearrange("p g r -> p (g r)"),
+                in_=grouped[:],
+            )
+            return codes, scales
+
+        def add_bias(gate_index, half):
+            first = gate_index * OUT + half * BLOCK
+            pre = gate_pool.tile(
+                [P, BATCH_TILES, BLOCK], F32, name="pre_%s%d" % (GATES[gate_index], half)
+            )
+            nc.vector.tensor_tensor(
+                out=pre[:],
+                in0=xg_parts[(gate_index, half)][:],
+                in1=bias_all[:, first : first + BLOCK]
+                .unsqueeze(1)
+                .to_broadcast([P, BATCH_TILES, BLOCK]),
+                op=ALU.add,
+            )
+            return pre
+
+        quantised = {
+            "hx": quantise_block(hx_raw, const, "hx"),
+            "cx": quantise_block(cx_raw, const, "cx"),
+        }
+
+        pres = {}
+        accs = {}
+        ready = quantise_block(blocks[0][3], weight_pool, "w")
+        for n, (half, gate_index, act_name, raw, opens, closes) in enumerate(blocks):
+            w_codes, w_scales = ready
+            if opens:
+                pres[gate_index] = add_bias(gate_index, half)
+            if n + 1 < len(blocks):
+                ready = quantise_block(blocks[n + 1][3], weight_pool, "w")
+            act_codes, act_scales = quantised[act_name]
+            for t in range(BATCH_TILES):
+                if opens:
+                    accs[t] = acc_psum.tile([P, BLOCK], F32, name="acc")
+                rows = slice(t * P, (t + 1) * P)
+                for g in range(PASSES):
+                    nc.tensor.matmul_mx(
+                        out=accs[t][:],
+                        lhsT=act_codes[:, g, rows].bitcast(FP8X4),
+                        lhsT_scale=act_scales[:, g, rows],
+                        rhs=w_codes[:, g, :].bitcast(FP8X4),
+                        rhs_scale=w_scales[:, g, :],
+                        start=(opens and g == 0),
+                        stop=(closes and g == PASSES - 1),
+                    )
+            if not closes:
+                continue
+            pre = pres[gate_index]
+            func = ACT.Tanh if GATES[gate_index] == "g" else ACT.Sigmoid
+            cols = slice(half * BLOCK, (half + 1) * BLOCK)
+            for t in range(BATCH_TILES):
+                nc.vector.tensor_tensor(out=pre[:, t, :], in0=accs[t][:], in1=pre[:, t, :], op=ALU.add)
+                nc.scalar.activation(out=pre[:, t, :], in_=pre[:, t, :], func=func)
+            if GATES[gate_index] == "f":
+                cx_rows = cx_raw[:].rearrange("p (t k) -> p t k", t=BATCH_TILES)
+                for t in range(BATCH_TILES):
+                    nc.vector.scalar_tensor_tensor(
+                        out=pre[:, t, :], in0=pre[:, t, :], scalar=decay[:, t : t + 1],
+                        in1=cx_rows[:, t, cols], op0=ALU.mult, op1=ALU.mult,
+                    )
+            if GATES[gate_index] == "g":
+                gate_i, gate_f = pres[0], pres[1]
+                for t in range(BATCH_TILES):
+                    nc.vector.scalar_tensor_tensor(
+                        out=gate_i[:, t, :], in0=gate_i[:, t, :],
+                        scalar=decay[:, BATCH_TILES + t : BATCH_TILES + t + 1],
+                        in1=pre[:, t, :], op0=ALU.mult, op1=ALU.mult,
+                    )
+                    nc.vector.tensor_tensor(
+                        out=gate_i[:, t, :], in0=gate_i[:, t, :], in1=gate_f[:, t, :], op=ALU.add
+                    )
+                    nc.sync.dma_start(out=out[t * P : (t + 1) * P, cols], in_=gate_i[:, t, :])

@@ -5,6 +5,7 @@ from concourse.masks import make_identity
 
 F32 = mybir.dt.float32
 BF16 = mybir.dt.bfloat16
+I32 = mybir.dt.int32
 U32 = mybir.dt.uint32
 U8 = mybir.dt.uint8
 FP8X4 = mybir.dt.float8_e4m3fn_x4
@@ -15,7 +16,6 @@ P = 128
 B = 512
 K = 1024
 OUT = 1024
-GATES = ("i", "f", "g")
 K_PASS = 512
 PASSES = K // K_PASS
 BLOCK = 512
@@ -23,6 +23,8 @@ ROW_TILES = BLOCK // P
 BATCH_TILES = B // P
 HALVES = OUT // BLOCK
 WORDS = K // 2
+GATE_COLUMN = {"i": 0, "f": OUT, "g": 2 * OUT}
+GATE_ORDER = ("f", "i", "g")
 
 FLOPS = 2 * B * K * (3 * OUT + 2 * OUT)
 
@@ -41,10 +43,14 @@ def tile_ircnn_lstmcell_pa_kernel(
         acc_psum = ctx.enter_context(tc.psum_pool(name="acc", bufs=4))
 
         bias_row = const.tile([P, 3 * OUT], BF16, name="bias_row")
-        nc.vector.memset(bias_row[:], 0.0)
-        nc.scalar.dma_start(out=bias_row[0:1, :], in_=b_hh.rearrange("(o c) -> o c", o=1))
+        nc.vector.memset(bias_row[:].bitcast(I32), 0)
+        nc.sync.dma_start(out=bias_row[0:1, :], in_=b_hh.rearrange("(o c) -> o c", o=1))
         td_rows = const.tile([P, P], BF16, name="td_rows")
         nc.vector.memset(td_rows[:], 0.0)
+        a_bf = const.tile([P, 1], BF16, name="a_bf")
+        nc.scalar.dma_start(out=a_bf[:], in_=a.partition_broadcast(P))
+        b_bf = const.tile([P, 1], BF16, name="b_bf")
+        nc.scalar.dma_start(out=b_bf[:], in_=b.partition_broadcast(P))
         nc.scalar.dma_start(
             out=td_rows[0:BATCH_TILES, :], in_=td0.rearrange("(t p) -> t p", p=P)
         )
@@ -52,10 +58,6 @@ def tile_ircnn_lstmcell_pa_kernel(
             out=td_rows[BATCH_TILES : 2 * BATCH_TILES, :],
             in_=td1.rearrange("(t p) -> t p", p=P),
         )
-        a_bf = const.tile([P, 1], BF16, name="a_bf")
-        nc.scalar.dma_start(out=a_bf[:], in_=a.partition_broadcast(P))
-        b_bf = const.tile([P, 1], BF16, name="b_bf")
-        nc.scalar.dma_start(out=b_bf[:], in_=b.partition_broadcast(P))
 
         def load_block(rows, pool, name):
             raw = pool.tile([P, ROW_TILES * K], BF16, name=name)
@@ -65,63 +67,43 @@ def tile_ircnn_lstmcell_pa_kernel(
             )
             return raw
 
-        def load_xg(gate_index, half):
-            first = gate_index * OUT + half * BLOCK
-            xg_part = gate_pool.tile(
-                [P, BATCH_TILES, BLOCK], BF16, name="xg_%s%d" % (GATES[gate_index], half)
-            )
+        def load_xg(gate, half):
+            first = GATE_COLUMN[gate] + half * BLOCK
+            xg_part = gate_pool.tile([P, BATCH_TILES, BLOCK], BF16, name="xg_%s%d" % (gate, half))
             nc.sync.dma_start(
                 out=xg_part[:],
                 in_=xg[:, first : first + BLOCK].rearrange("(t p) c -> p t c", p=P),
             )
             return xg_part
 
-        hx_raw = load_block(hx, raw_pool, "raw")
-        cx_raw = load_block(cx, const, "cx_raw")
         peephole = {"i": w_pi, "f": w_pf}
         blocks = []
-        xg_parts = {}
+        parts = []
         for half in range(HALVES):
-            for gate_index, gate in enumerate(GATES):
-                first = gate_index * OUT + half * BLOCK
-                has_peephole = gate in peephole
-                blocks.append(
-                    (half, gate_index, "hx",
-                     load_block(w_hh[first : first + BLOCK, :], raw_pool, "raw"),
-                     True, not has_peephole)
-                )
-                xg_parts[(gate_index, half)] = load_xg(gate_index, half)
-                if has_peephole:
+            for gate in GATE_ORDER:
+                first = GATE_COLUMN[gate] + half * BLOCK
+                parts.append((gate, half))
+                blocks.append((gate, half, "hx", w_hh[first : first + BLOCK, :], True, gate == "g"))
+                if gate != "g":
                     rows = peephole[gate][half * BLOCK : (half + 1) * BLOCK, :]
-                    blocks.append(
-                        (half, gate_index, "cx", load_block(rows, raw_pool, "raw"), False, True)
-                    )
+                    blocks.append((gate, half, "cx", rows, False, True))
+
+        xg_parts = {}
+        raws = {}
+        large = [("hx", hx), (0, blocks[0][3]), ("cx", cx)]
+        large.extend([(n, blocks[n][3]) for n in range(1, len(blocks))])
+        for position, (key, rows) in enumerate(large):
+            if key == "cx":
+                raws[key] = load_block(rows, const, "cx_raw")
+            else:
+                raws[key] = load_block(rows, raw_pool, "raw")
+            if position < len(parts):
+                xg_parts[parts[position]] = load_xg(parts[position][0], parts[position][1])
 
         ident = const.tile([P, P], F32, name="ident")
         make_identity(nc, ident[:])
         ones = const.tile([P, P], BF16, name="ones")
         nc.vector.memset(ones[:], 1.0)
-
-        bias_all = const.tile([P, 3 * OUT], BF16, name="bias_all")
-        for c in range(3 * OUT // BLOCK):
-            cols = slice(c * BLOCK, (c + 1) * BLOCK)
-            spread = flip_psum.tile([P, BLOCK], F32, name="spread", tag="flip")
-            nc.tensor.matmul(out=spread[:], lhsT=ones[:], rhs=bias_row[:, cols], start=True, stop=True)
-            nc.scalar.copy(out=bias_all[:, cols], in_=spread[:])
-
-        td_rows32 = const.tile([P, P], F32, name="td_rows32")
-        nc.vector.tensor_copy(out=td_rows32[:], in_=td_rows[:])
-        td_cols = flip_psum.tile([P, P], F32, name="td_cols", tag="flip")
-        nc.tensor.transpose(td_cols[:], td_rows32[:], ident[:])
-        minus_b = const.tile([P, 1], F32, name="minus_b")
-        nc.vector.tensor_scalar_mul(out=minus_b[:], in0=b_bf[:], scalar1=-1.0)
-        a_f32 = const.tile([P, 1], F32, name="a_f32")
-        nc.vector.tensor_copy(out=a_f32[:], in_=a_bf[:])
-        decay = const.tile([P, 2 * BATCH_TILES], F32, name="decay")
-        nc.scalar.activation(
-            out=decay[:], in_=td_cols[:, 0 : 2 * BATCH_TILES], func=ACT.Exp, scale=minus_b[:, 0:1]
-        )
-        nc.vector.tensor_scalar_mul(out=decay[:], in0=decay[:], scalar1=a_f32[:, 0:1])
 
         def quantise_block(raw, pool, name):
             words = raw[:].bitcast(F32)
@@ -147,14 +129,23 @@ def tile_ircnn_lstmcell_pa_kernel(
             )
             return codes, scales
 
-        def add_bias(gate_index, half):
-            first = gate_index * OUT + half * BLOCK
-            pre = gate_pool.tile(
-                [P, BATCH_TILES, BLOCK], F32, name="pre_%s%d" % (GATES[gate_index], half)
-            )
+        quantised = {"hx": quantise_block(raws["hx"], const, "hx")}
+        ready = quantise_block(raws[0], weight_pool, "w")
+
+        bias_all = const.tile([P, 3 * OUT], BF16, name="bias_all")
+        for gate, half in parts:
+            first = GATE_COLUMN[gate] + half * BLOCK
+            cols = slice(first, first + BLOCK)
+            spread = flip_psum.tile([P, BLOCK], F32, name="spread", tag="flip")
+            nc.tensor.matmul(out=spread[:], lhsT=ones[:], rhs=bias_row[:, cols], start=True, stop=True)
+            nc.scalar.copy(out=bias_all[:, cols], in_=spread[:])
+
+        def add_bias(gate, half):
+            first = GATE_COLUMN[gate] + half * BLOCK
+            pre = gate_pool.tile([P, BATCH_TILES, BLOCK], F32, name="pre_%s%d" % (gate, half))
             nc.vector.tensor_tensor(
                 out=pre[:],
-                in0=xg_parts[(gate_index, half)][:],
+                in0=xg_parts[(gate, half)][:],
                 in1=bias_all[:, first : first + BLOCK]
                 .unsqueeze(1)
                 .to_broadcast([P, BATCH_TILES, BLOCK]),
@@ -162,30 +153,39 @@ def tile_ircnn_lstmcell_pa_kernel(
             )
             return pre
 
-        quantised = {
-            "hx": quantise_block(hx_raw, const, "hx"),
-            "cx": quantise_block(cx_raw, const, "cx"),
-        }
+        quantised["cx"] = quantise_block(raws["cx"], const, "cx")
+
+        td_rows32 = const.tile([P, P], F32, name="td_rows32")
+        nc.vector.tensor_copy(out=td_rows32[:], in_=td_rows[:])
+        td_cols = flip_psum.tile([P, P], F32, name="td_cols", tag="flip")
+        nc.tensor.transpose(td_cols[:], td_rows32[:], ident[:])
+        minus_b = const.tile([P, 1], F32, name="minus_b")
+        nc.vector.tensor_scalar_mul(out=minus_b[:], in0=b_bf[:], scalar1=-1.0)
+        a_f32 = const.tile([P, 1], F32, name="a_f32")
+        nc.vector.tensor_copy(out=a_f32[:], in_=a_bf[:])
+        decay = const.tile([P, 2 * BATCH_TILES], F32, name="decay")
+        nc.scalar.activation(
+            out=decay[:], in_=td_cols[:, 0 : 2 * BATCH_TILES], func=ACT.Exp, scale=minus_b[:, 0:1]
+        )
+        nc.vector.tensor_scalar_mul(out=decay[:], in0=decay[:], scalar1=a_f32[:, 0:1])
+        cx_rows = raws["cx"][:].rearrange("p (t k) -> p t k", t=BATCH_TILES)
 
         pres = {}
         accs = {}
-        ready = quantise_block(blocks[0][3], weight_pool, "w")
-        for n, (half, gate_index, act_name, raw, opens, closes) in enumerate(blocks):
+        for n, (gate, half, act_name, rows, opens, closes) in enumerate(blocks):
             w_codes, w_scales = ready
-            if opens:
-                pres[gate_index] = add_bias(gate_index, half)
             if n + 1 < len(blocks):
-                ready = quantise_block(blocks[n + 1][3], weight_pool, "w")
+                ready = quantise_block(raws[n + 1], weight_pool, "w")
             act_codes, act_scales = quantised[act_name]
             for t in range(BATCH_TILES):
                 if opens:
                     accs[t] = acc_psum.tile([P, BLOCK], F32, name="acc")
-                rows = slice(t * P, (t + 1) * P)
+                batch = slice(t * P, (t + 1) * P)
                 for g in range(PASSES):
                     nc.tensor.matmul_mx(
                         out=accs[t][:],
-                        lhsT=act_codes[:, g, rows].bitcast(FP8X4),
-                        lhsT_scale=act_scales[:, g, rows],
+                        lhsT=act_codes[:, g, batch].bitcast(FP8X4),
+                        lhsT_scale=act_scales[:, g, batch],
                         rhs=w_codes[:, g, :].bitcast(FP8X4),
                         rhs_scale=w_scales[:, g, :],
                         start=(opens and g == 0),
@@ -193,21 +193,21 @@ def tile_ircnn_lstmcell_pa_kernel(
                     )
             if not closes:
                 continue
-            pre = pres[gate_index]
-            func = ACT.Tanh if GATES[gate_index] == "g" else ACT.Sigmoid
+            pre = add_bias(gate, half)
+            pres[gate] = pre
+            func = ACT.Tanh if gate == "g" else ACT.Sigmoid
             cols = slice(half * BLOCK, (half + 1) * BLOCK)
             for t in range(BATCH_TILES):
                 nc.vector.tensor_tensor(out=pre[:, t, :], in0=accs[t][:], in1=pre[:, t, :], op=ALU.add)
                 nc.scalar.activation(out=pre[:, t, :], in_=pre[:, t, :], func=func)
-            if GATES[gate_index] == "f":
-                cx_rows = cx_raw[:].rearrange("p (t k) -> p t k", t=BATCH_TILES)
+            if gate == "f":
                 for t in range(BATCH_TILES):
                     nc.vector.scalar_tensor_tensor(
                         out=pre[:, t, :], in0=pre[:, t, :], scalar=decay[:, t : t + 1],
                         in1=cx_rows[:, t, cols], op0=ALU.mult, op1=ALU.mult,
                     )
-            if GATES[gate_index] == "g":
-                gate_i, gate_f = pres[0], pres[1]
+            if gate == "g":
+                gate_i, gate_f = pres["i"], pres["f"]
                 for t in range(BATCH_TILES):
                     nc.vector.scalar_tensor_tensor(
                         out=gate_i[:, t, :], in0=gate_i[:, t, :],

@@ -21,12 +21,12 @@ PASSES = K // K_PASS
 BLOCK = 512
 ROW_TILES = BLOCK // P
 BATCH_TILES = B // P
-HALVES = OUT // BLOCK
 WORDS = K // 2
 GATE_COLUMN = {"i": 0, "f": OUT, "g": 2 * OUT}
-GATE_ORDER = ("f", "i", "g")
 
 FLOPS = 2 * B * K * (3 * OUT + 2 * OUT)
+
+PARTS = (("g", 0), ("g", 1), ("f", 0), ("i", 0), ("f", 1), ("i", 1))
 
 
 def tile_ircnn_lstmcell_pa_kernel(
@@ -35,155 +35,167 @@ def tile_ircnn_lstmcell_pa_kernel(
     nc = tc.nc
     with ExitStack() as ctx:
         const = ctx.enter_context(tc.tile_pool(name="const", bufs=1))
-        raw_pool = ctx.enter_context(tc.tile_pool(name="raw", bufs=7))
+        raw_pool = ctx.enter_context(tc.tile_pool(name="raw", bufs=11))
         grouped_pool = ctx.enter_context(tc.tile_pool(name="grouped", bufs=3))
         weight_pool = ctx.enter_context(tc.tile_pool(name="weight", bufs=3))
         gate_pool = ctx.enter_context(tc.tile_pool(name="gate", bufs=1))
         flip_psum = ctx.enter_context(tc.psum_pool(name="flip", bufs=4))
         acc_psum = ctx.enter_context(tc.psum_pool(name="acc", bufs=4))
+        ctx.enter_context(tc.manual_schedule())
 
-        bias_row = const.tile([P, 3 * OUT], BF16, name="bias_row")
-        nc.vector.memset(bias_row[:].bitcast(I32), 0)
-        nc.sync.dma_start(out=bias_row[0:1, :], in_=b_hh.rearrange("(o c) -> o c", o=1))
-        td_rows = const.tile([P, P], BF16, name="td_rows")
-        nc.vector.memset(td_rows[:], 0.0)
-        a_bf = const.tile([P, 1], BF16, name="a_bf")
-        nc.scalar.dma_start(out=a_bf[:], in_=a.partition_broadcast(P))
-        b_bf = const.tile([P, 1], BF16, name="b_bf")
-        nc.scalar.dma_start(out=b_bf[:], in_=b.partition_broadcast(P))
-        nc.scalar.dma_start(
-            out=td_rows[0:BATCH_TILES, :], in_=td0.rearrange("(t p) -> t p", p=P)
-        )
-        nc.scalar.dma_start(
-            out=td_rows[BATCH_TILES : 2 * BATCH_TILES, :],
-            in_=td1.rearrange("(t p) -> t p", p=P),
-        )
-
-        def load_block(rows, pool, name):
-            raw = pool.tile([P, ROW_TILES * K], BF16, name=name)
+        bias_rows = {}
+        for gates, first, engine in (("g", 2 * OUT, nc.vector), ("if", 0, nc.gpsimd)):
+            width = OUT * len(gates)
+            row = const.tile([P, width], BF16, name="bias_rows_" + gates)
+            engine.memset(row[:].bitcast(I32), 0)
             nc.sync.dma_start(
-                out=raw[:].rearrange("p (j k) -> p j k", j=ROW_TILES),
-                in_=rows.rearrange("(j p) k -> p j k", p=P),
+                out=row[0:1, :], in_=b_hh[first : first + width].rearrange("(o c) -> o c", o=1)
             )
-            return raw
-
-        def load_xg(gate, half):
-            first = GATE_COLUMN[gate] + half * BLOCK
-            xg_part = gate_pool.tile([P, BATCH_TILES, BLOCK], BF16, name="xg_%s%d" % (gate, half))
-            nc.sync.dma_start(
-                out=xg_part[:],
-                in_=xg[:, first : first + BLOCK].rearrange("(t p) c -> p t c", p=P),
-            )
-            return xg_part
-
-        peephole = {"i": w_pi, "f": w_pf}
-        blocks = []
-        parts = []
-        for half in range(HALVES):
-            for gate in GATE_ORDER:
-                first = GATE_COLUMN[gate] + half * BLOCK
-                parts.append((gate, half))
-                blocks.append((gate, half, "hx", w_hh[first : first + BLOCK, :], True, gate == "g"))
-                if gate != "g":
-                    rows = peephole[gate][half * BLOCK : (half + 1) * BLOCK, :]
-                    blocks.append((gate, half, "cx", rows, False, True))
-
-        xg_parts = {}
-        raws = {}
-        large = [("hx", hx), (0, blocks[0][3]), ("cx", cx)]
-        large.extend([(n, blocks[n][3]) for n in range(1, len(blocks))])
-        for position, (key, rows) in enumerate(large):
-            if key == "cx":
-                raws[key] = load_block(rows, const, "cx_raw")
-            else:
-                raws[key] = load_block(rows, raw_pool, "raw")
-            if position < len(parts):
-                xg_parts[parts[position]] = load_xg(parts[position][0], parts[position][1])
-
+            for position, gate in enumerate(gates):
+                bias_rows[gate] = row[:, position * OUT : (position + 1) * OUT]
         ident = const.tile([P, P], F32, name="ident")
         make_identity(nc, ident[:])
         ones = const.tile([P, P], BF16, name="ones")
         nc.vector.memset(ones[:], 1.0)
+        warm = const.tile([P, 1], F32, name="warm")
+        nc.vector.memset(warm[:], 0.0)
+        nc.scalar.activation(out=warm[:], in_=warm[:], func=ACT.Exp)
+        b_bf = const.tile([P, 1], BF16, name="b_bf")
+        a_bf = const.tile([P, 1], BF16, name="a_bf")
+        td = const.tile([P, 2, 16], BF16, name="td")
 
-        def quantise_block(raw, pool, name):
-            words = raw[:].bitcast(F32)
-            grouped = grouped_pool.tile([P, PASSES * BLOCK * 4], BF16, name="grouped", align_bytes=64)
-            grouped_words = grouped[:].bitcast(F32).rearrange(
-                "p (g r u) -> p g r u", g=PASSES, u=2
-            )
+        def load_decay():
+            nc.sync.dma_start(out=b_bf[:], in_=b.partition_broadcast(P))
+            nc.sync.dma_start(out=a_bf[:], in_=a.partition_broadcast(P))
+            nc.sync.dma_start(out=td[:, 0, 0:BATCH_TILES], in_=td0.rearrange("(p t) -> p t", p=P))
+            nc.sync.dma_start(out=td[:, 1, 0:BATCH_TILES], in_=td1.rearrange("(p t) -> p t", p=P))
+
+        def load_rows(rows, pool, name, row_view, pieces):
+            raw = pool.tile([P, ROW_TILES, K], BF16, name=name)
+            source = rows.rearrange(row_view, p=P)
+            step = ROW_TILES // pieces
+            for j in range(0, ROW_TILES, step):
+                nc.sync.dma_start(out=raw[:, j : j + step, :], in_=source[:, j : j + step, :])
+            return raw
+
+        rows_of = {}
+        for gate, half in PARTS:
+            first = GATE_COLUMN[gate] + half * BLOCK
+            rows_of["w", gate, half] = w_hh[first : first + BLOCK, :]
+            if gate != "g":
+                peephole = w_pi if gate == "i" else w_pf
+                rows_of["p", gate, half] = peephole[half * BLOCK : (half + 1) * BLOCK, :]
+
+        xg_parts = {}
+
+        def load_xg(gate, half, pieces=1):
+            first = GATE_COLUMN[gate] + half * BLOCK
+            part = gate_pool.tile([P, BATCH_TILES, BLOCK], BF16, name="xg_%s%d" % (gate, half))
+            source = xg[:, first : first + BLOCK].rearrange("(p t) c -> p t c", p=P)
+            step = BATCH_TILES // pieces
+            for t in range(0, BATCH_TILES, step):
+                nc.sync.dma_start(out=part[:, t : t + step, :], in_=source[:, t : t + step, :])
+            xg_parts[gate, half] = part
+
+        raws = {}
+
+        def load_weight(key, pieces=1):
+            raws[key] = load_rows(rows_of[key], raw_pool, "raw", "(j p) k -> p j k", pieces)
+
+        load_xg("g", 0)
+        raws["hx"] = load_rows(hx, raw_pool, "raw", "(p j) k -> p j k", 2)
+        load_xg("g", 1)
+        load_weight(("w", "g", 0), 2)
+        load_xg("f", 0)
+        load_weight(("w", "g", 1))
+        raws["cx"] = load_rows(cx, const, "cx_raw", "(p j) k -> p j k", 1)
+        load_xg("i", 0)
+        load_decay()
+        load_weight(("w", "f", 0))
+        load_weight(("p", "f", 0))
+        load_xg("f", 1)
+        load_weight(("w", "i", 0))
+        load_xg("i", 1)
+        load_weight(("p", "i", 0))
+        load_weight(("w", "f", 1))
+        load_weight(("p", "f", 1))
+        load_weight(("w", "i", 1))
+        load_weight(("p", "i", 1))
+
+        flipped = {}
+        grouped = {}
+        quantised = {}
+        spreads = {}
+        pre = {}
+        accs = {}
+
+        def transpose_block(key):
+            words = raws[key][:].rearrange("p j k -> p (j k)").bitcast(F32)
             for j in range(ROW_TILES):
-                flipped = flip_psum.tile([P, 2 * PASSES, P], F32, name="flipped", tag="flip")
+                bank = flip_psum.tile([P, 2 * PASSES, P], F32, name="flipped", tag="flip")
                 for q in range(2 * PASSES):
                     first = j * WORDS + q * P
-                    nc.tensor.transpose(flipped[:, q, :], words[:, first : first + P], ident[:])
+                    nc.tensor.transpose(bank[:, q, :], words[:, first : first + P], ident[:])
+                flipped[key, j] = bank
+
+        def group_block(key):
+            tile = grouped_pool.tile([P, PASSES * BLOCK * 4], BF16, name="grouped", align_bytes=64)
+            target = tile[:].bitcast(F32).rearrange("p (g r u) -> p g r u", g=PASSES, u=2)
+            for j in range(ROW_TILES):
                 nc.scalar.copy(
-                    out=grouped_words[:, :, j * P : (j + 1) * P, :],
-                    in_=flipped[:].rearrange("p (g u) r -> p g r u", u=2),
+                    out=target[:, :, j * P : (j + 1) * P, :],
+                    in_=flipped[key, j][:].rearrange("p (g u) r -> p g r u", u=2),
                 )
+            grouped[key] = tile
+
+        def quantise_block(key):
+            pool, name = (const, key) if key in ("hx", "cx") else (weight_pool, "w")
             codes = pool.tile([P, PASSES, BLOCK], U32, name=name + "_codes", align_bytes=64)
             scales = pool.tile([P, PASSES, BLOCK], U8, name=name + "_scales", align_bytes=64)
             nc.vector.quantize_mx(
                 out=codes[:].rearrange("p g r -> p (g r)").bitcast(FP8X4),
                 scales=scales[:].rearrange("p g r -> p (g r)"),
-                in_=grouped[:],
+                in_=grouped[key][:],
             )
-            return codes, scales
+            quantised[key] = (codes, scales)
 
-        quantised = {"hx": quantise_block(raws["hx"], const, "hx")}
-        ready = quantise_block(raws[0], weight_pool, "w")
-
-        bias_all = const.tile([P, 3 * OUT], BF16, name="bias_all")
-        for gate, half in parts:
-            first = GATE_COLUMN[gate] + half * BLOCK
-            cols = slice(first, first + BLOCK)
-            spread = flip_psum.tile([P, BLOCK], F32, name="spread", tag="flip")
-            nc.tensor.matmul(out=spread[:], lhsT=ones[:], rhs=bias_row[:, cols], start=True, stop=True)
-            nc.scalar.copy(out=bias_all[:, cols], in_=spread[:])
-
-        def add_bias(gate, half):
-            first = GATE_COLUMN[gate] + half * BLOCK
-            pre = gate_pool.tile([P, BATCH_TILES, BLOCK], F32, name="pre_%s%d" % (gate, half))
-            nc.vector.tensor_tensor(
-                out=pre[:],
-                in0=xg_parts[(gate, half)][:],
-                in1=bias_all[:, first : first + BLOCK]
-                .unsqueeze(1)
-                .to_broadcast([P, BATCH_TILES, BLOCK]),
-                op=ALU.add,
+        def spread_bias(gate, half, pool, tag):
+            bank = pool.tile([P, BLOCK], F32, name="spread", tag=tag)
+            nc.tensor.matmul(
+                out=bank[:],
+                lhsT=ones[:],
+                rhs=bias_rows[gate][:, half * BLOCK : (half + 1) * BLOCK],
+                start=True,
+                stop=True,
             )
-            return pre
+            spreads[gate, half] = bank
 
-        quantised["cx"] = quantise_block(raws["cx"], const, "cx")
+        def add_bias(gate, half, pairs):
+            if (gate, half) not in pre:
+                pre[gate, half] = gate_pool.tile(
+                    [P, BATCH_TILES, BLOCK], F32, name="pre_%s%d" % (gate, half)
+                )
+            for pair in pairs:
+                rows = slice(2 * pair, 2 * pair + 2)
+                nc.vector.tensor_tensor(
+                    out=pre[gate, half][:, rows, :],
+                    in0=xg_parts[gate, half][:, rows, :],
+                    in1=spreads[gate, half][:].unsqueeze(1).to_broadcast([P, 2, BLOCK]),
+                    op=ALU.add,
+                )
 
-        td_rows32 = const.tile([P, P], F32, name="td_rows32")
-        nc.vector.tensor_copy(out=td_rows32[:], in_=td_rows[:])
-        td_cols = flip_psum.tile([P, P], F32, name="td_cols", tag="flip")
-        nc.tensor.transpose(td_cols[:], td_rows32[:], ident[:])
-        minus_b = const.tile([P, 1], F32, name="minus_b")
-        nc.vector.tensor_scalar_mul(out=minus_b[:], in0=b_bf[:], scalar1=-1.0)
-        a_f32 = const.tile([P, 1], F32, name="a_f32")
-        nc.vector.tensor_copy(out=a_f32[:], in_=a_bf[:])
-        decay = const.tile([P, 2 * BATCH_TILES], F32, name="decay")
-        nc.scalar.activation(
-            out=decay[:], in_=td_cols[:, 0 : 2 * BATCH_TILES], func=ACT.Exp, scale=minus_b[:, 0:1]
-        )
-        nc.vector.tensor_scalar_mul(out=decay[:], in0=decay[:], scalar1=a_f32[:, 0:1])
-        cx_rows = raws["cx"][:].rearrange("p (t k) -> p t k", t=BATCH_TILES)
-
-        pres = {}
-        accs = {}
-        for n, (gate, half, act_name, rows, opens, closes) in enumerate(blocks):
-            w_codes, w_scales = ready
-            if n + 1 < len(blocks):
-                ready = quantise_block(raws[n + 1], weight_pool, "w")
-            act_codes, act_scales = quantised[act_name]
+        def multiply(kind, gate, half):
+            act_codes, act_scales = quantised["hx" if kind == "w" else "cx"]
+            w_codes, w_scales = quantised[kind, gate, half]
+            opens = kind == "w"
+            closes = kind == "p" or gate == "g"
             for t in range(BATCH_TILES):
                 if opens:
-                    accs[t] = acc_psum.tile([P, BLOCK], F32, name="acc")
+                    accs[gate, half, t] = acc_psum.tile([P, BLOCK], F32, name="acc", tag="acc")
                 batch = slice(t * P, (t + 1) * P)
                 for g in range(PASSES):
                     nc.tensor.matmul_mx(
-                        out=accs[t][:],
+                        out=accs[gate, half, t][:],
                         lhsT=act_codes[:, g, batch].bitcast(FP8X4),
                         lhsT_scale=act_scales[:, g, batch],
                         rhs=w_codes[:, g, :].bitcast(FP8X4),
@@ -191,30 +203,152 @@ def tile_ircnn_lstmcell_pa_kernel(
                         start=(opens and g == 0),
                         stop=(closes and g == PASSES - 1),
                     )
-            if not closes:
-                continue
-            pre = add_bias(gate, half)
-            pres[gate] = pre
+
+        def finish_gate(gate, half):
             func = ACT.Tanh if gate == "g" else ACT.Sigmoid
-            cols = slice(half * BLOCK, (half + 1) * BLOCK)
+            tile = pre[gate, half]
             for t in range(BATCH_TILES):
-                nc.vector.tensor_tensor(out=pre[:, t, :], in0=accs[t][:], in1=pre[:, t, :], op=ALU.add)
-                nc.scalar.activation(out=pre[:, t, :], in_=pre[:, t, :], func=func)
-            if gate == "f":
-                for t in range(BATCH_TILES):
-                    nc.vector.scalar_tensor_tensor(
-                        out=pre[:, t, :], in0=pre[:, t, :], scalar=decay[:, t : t + 1],
-                        in1=cx_rows[:, t, cols], op0=ALU.mult, op1=ALU.mult,
-                    )
-            if gate == "g":
-                gate_i, gate_f = pres["i"], pres["f"]
-                for t in range(BATCH_TILES):
-                    nc.vector.scalar_tensor_tensor(
-                        out=gate_i[:, t, :], in0=gate_i[:, t, :],
-                        scalar=decay[:, BATCH_TILES + t : BATCH_TILES + t + 1],
-                        in1=pre[:, t, :], op0=ALU.mult, op1=ALU.mult,
-                    )
-                    nc.vector.tensor_tensor(
-                        out=gate_i[:, t, :], in0=gate_i[:, t, :], in1=gate_f[:, t, :], op=ALU.add
-                    )
-                    nc.sync.dma_start(out=out[t * P : (t + 1) * P, cols], in_=gate_i[:, t, :])
+                nc.vector.tensor_tensor(
+                    out=tile[:, t, :], in0=accs[gate, half, t][:], in1=tile[:, t, :], op=ALU.add
+                )
+                nc.scalar.activation(out=tile[:, t, :], in_=tile[:, t, :], func=func)
+
+        def scale_f(half):
+            tile = pre["f", half]
+            for t in range(BATCH_TILES):
+                nc.vector.scalar_tensor_tensor(
+                    out=tile[:, t, :], in0=tile[:, t, :], scalar=decay[:, 0, t : t + 1],
+                    in1=raws["cx"][:, t, half * BLOCK : (half + 1) * BLOCK],
+                    op0=ALU.mult, op1=ALU.mult,
+                )
+
+        def scale_i(half, tiles):
+            tile = pre["i", half]
+            for t in tiles:
+                nc.vector.scalar_tensor_tensor(
+                    out=tile[:, t, :], in0=tile[:, t, :], scalar=decay[:, 1, t : t + 1],
+                    in1=pre["g", half][:, t, :], op0=ALU.mult, op1=ALU.mult,
+                )
+
+        out_rows = out.rearrange("(p t) c -> p t c", p=P)
+
+        def add_and_store(half, tiles):
+            tile = pre["i", half]
+            for t in tiles:
+                nc.vector.tensor_tensor(
+                    out=tile[:, t, :], in0=tile[:, t, :], in1=pre["f", half][:, t, :], op=ALU.add
+                )
+                nc.sync.dma_start(
+                    out=out_rows[:, t, half * BLOCK : (half + 1) * BLOCK], in_=tile[:, t, :]
+                )
+
+        def take_in(key):
+            transpose_block(key)
+            group_block(key)
+
+        def keep_bias(gate, half):
+            spread_bias(gate, half, flip_psum, "flip")
+            kept = const.tile([P, BLOCK], BF16, name="bias_%s%d" % (gate, half))
+            nc.scalar.copy(out=kept[:], in_=spreads[gate, half][:])
+            spreads[gate, half] = kept
+
+        def add_bias_aside(gate, half, tiles):
+            if (gate, half) not in pre:
+                pre[gate, half] = gate_pool.tile(
+                    [P, BATCH_TILES, BLOCK], F32, name="pre_%s%d" % (gate, half)
+                )
+            for t in tiles:
+                nc.gpsimd.tensor_tensor(
+                    out=pre[gate, half][:, t, :], in0=xg_parts[gate, half][:, t, :],
+                    in1=spreads[gate, half][:], op=ALU.add,
+                )
+
+        def make_decay():
+            minus_b = const.tile([P, 1], F32, name="minus_b")
+            nc.vector.tensor_scalar_mul(out=minus_b[:], in0=b_bf[:], scalar1=-1.0)
+            nc.scalar.activation(
+                out=decay[:], in_=td[:, :, 0:BATCH_TILES], func=ACT.Exp, scale=minus_b[:, 0:1]
+            )
+
+        decay = const.tile([P, 2, BATCH_TILES], F32, name="decay")
+        spread_bias("g", 0, acc_psum, "acc")
+        spread_bias("g", 1, acc_psum, "acc")
+        spread_bias("f", 0, acc_psum, "acc")
+        spread_bias("i", 0, acc_psum, "acc")
+        keep_bias("f", 1)
+        keep_bias("i", 1)
+
+        add_bias("g", 0, (0, 1))
+        take_in("hx")
+        add_bias("g", 1, (0, 1))
+        quantise_block("hx")
+        take_in(("w", "g", 0))
+        quantise_block(("w", "g", 0))
+
+        take_in(("w", "g", 1))
+        add_bias("f", 0, (0, 1))
+
+        multiply("w", "g", 0)
+        take_in("cx")
+        quantise_block(("w", "g", 1))
+        finish_gate("g", 0)
+
+        take_in(("w", "f", 0))
+        quantise_block("cx")
+        add_bias("i", 0, (0,))
+        multiply("w", "g", 1)
+        finish_gate("g", 1)
+
+        take_in(("p", "f", 0))
+        quantise_block(("w", "f", 0))
+        add_bias("i", 0, (1,))
+        add_bias("f", 1, (0,))
+        make_decay()
+
+        take_in(("w", "i", 0))
+        nc.scalar.activation(out=warm[:], in_=warm[:], func=ACT.Sigmoid)
+        quantise_block(("p", "f", 0))
+        add_bias("f", 1, (1,))
+        multiply("w", "f", 0)
+        nc.vector.tensor_scalar_mul(out=decay[:], in0=decay[:], scalar1=a_bf[:, 0:1])
+
+        take_in(("p", "i", 0))
+        quantise_block(("w", "i", 0))
+        multiply("p", "f", 0)
+        add_bias("i", 1, (0,))
+        finish_gate("f", 0)
+
+        take_in(("w", "f", 1))
+        quantise_block(("p", "i", 0))
+        scale_f(0)
+        multiply("w", "i", 0)
+
+        take_in(("p", "f", 1))
+        quantise_block(("w", "f", 1))
+        add_bias("i", 1, (1,))
+        multiply("p", "i", 0)
+        finish_gate("i", 0)
+
+        take_in(("w", "i", 1))
+        quantise_block(("p", "f", 1))
+        scale_i(0, range(BATCH_TILES))
+        multiply("w", "f", 1)
+
+        take_in(("p", "i", 1))
+        quantise_block(("w", "i", 1))
+        add_and_store(0, (0, 1,))
+        multiply("p", "f", 1)
+        finish_gate("f", 1)
+
+        quantise_block(("p", "i", 1))
+        add_and_store(0, (2, 3,))
+        scale_f(1)
+        multiply("w", "i", 1)
+        multiply("p", "i", 1)
+        finish_gate("i", 1)
+        scale_i(1, (0, 1,))
+        add_and_store(1, (0,))
+        scale_i(1, (2,))
+        add_and_store(1, (1,))
+        scale_i(1, (3,))
+        add_and_store(1, (2, 3,))

@@ -20,13 +20,12 @@ K_PASS = 512
 PASSES = K // K_PASS
 BLOCK = 512
 ROW_TILES = BLOCK // P
+QUARTER = 256
 BATCH_TILES = B // P
 WORDS = K // 2
 GATE_COLUMN = {"i": 0, "f": OUT, "g": 2 * OUT}
 
 FLOPS = 2 * B * K * (3 * OUT + 2 * OUT)
-
-PARTS = (("g", 0), ("g", 1), ("f", 0), ("i", 0), ("f", 1), ("i", 1))
 
 
 def tile_ircnn_lstmcell_pa_kernel(
@@ -63,6 +62,7 @@ def tile_ircnn_lstmcell_pa_kernel(
         b_bf = const.tile([P, 1], BF16, name="b_bf")
         a_bf = const.tile([P, 1], BF16, name="a_bf")
         td = const.tile([P, 2, 16], BF16, name="td")
+        decay = const.tile([P, 2, BATCH_TILES], F32, name="decay")
 
         def load_decay():
             nc.sync.dma_start(out=b_bf[:], in_=b.partition_broadcast(P))
@@ -70,57 +70,63 @@ def tile_ircnn_lstmcell_pa_kernel(
             nc.sync.dma_start(out=td[:, 0, 0:BATCH_TILES], in_=td0.rearrange("(p t) -> p t", p=P))
             nc.sync.dma_start(out=td[:, 1, 0:BATCH_TILES], in_=td1.rearrange("(p t) -> p t", p=P))
 
-        def load_rows(rows, pool, name, row_view, pieces):
-            raw = pool.tile([P, ROW_TILES, K], BF16, name=name)
-            source = rows.rearrange(row_view, p=P)
+        raws = {}
+
+        def load_activations(key, source, pool, pieces):
+            raw = pool.tile([P, ROW_TILES, K], BF16, name="raw" if pool is raw_pool else key + "_raw")
+            rows = source.rearrange("(p j) k -> p j k", p=P)
             step = ROW_TILES // pieces
             for j in range(0, ROW_TILES, step):
-                nc.sync.dma_start(out=raw[:, j : j + step, :], in_=source[:, j : j + step, :])
-            return raw
+                nc.sync.dma_start(out=raw[:, j : j + step, :], in_=rows[:, j : j + step, :])
+            raws[key] = raw
 
-        rows_of = {}
-        for gate, half in PARTS:
-            first = GATE_COLUMN[gate] + half * BLOCK
-            rows_of["w", gate, half] = w_hh[first : first + BLOCK, :]
-            if gate != "g":
+        def load_weights(gate, number):
+            raw = raw_pool.tile([P, ROW_TILES, K], BF16, name="raw")
+            if gate == "g":
+                pieces = [(w_hh, 2 * OUT + (2 * number + n) * QUARTER) for n in range(2)]
+            else:
                 peephole = w_pi if gate == "i" else w_pf
-                rows_of["p", gate, half] = peephole[half * BLOCK : (half + 1) * BLOCK, :]
+                pieces = [
+                    (w_hh, GATE_COLUMN[gate] + number * QUARTER),
+                    (peephole, number * QUARTER),
+                ]
+            for n, (source, first) in enumerate(pieces):
+                nc.sync.dma_start(
+                    out=raw[:, 2 * n : 2 * n + 2, :],
+                    in_=source[first : first + QUARTER, :].rearrange("(j p) k -> p j k", p=P),
+                )
+            raws[gate, number] = raw
 
         xg_parts = {}
 
-        def load_xg(gate, half, pieces=1):
-            first = GATE_COLUMN[gate] + half * BLOCK
-            part = gate_pool.tile([P, BATCH_TILES, BLOCK], BF16, name="xg_%s%d" % (gate, half))
-            source = xg[:, first : first + BLOCK].rearrange("(p t) c -> p t c", p=P)
-            step = BATCH_TILES // pieces
-            for t in range(0, BATCH_TILES, step):
-                nc.sync.dma_start(out=part[:, t : t + step, :], in_=source[:, t : t + step, :])
+        def load_xg(gate, half):
+            first = GATE_COLUMN[gate] + half * 2 * QUARTER
+            part = gate_pool.tile([P, BATCH_TILES, 2 * QUARTER], BF16, name="xg_%s%d" % (gate, half))
+            nc.sync.dma_start(
+                out=part[:],
+                in_=xg[:, first : first + 2 * QUARTER].rearrange("(p t) c -> p t c", p=P),
+            )
             xg_parts[gate, half] = part
 
-        raws = {}
-
-        def load_weight(key, pieces=1):
-            raws[key] = load_rows(rows_of[key], raw_pool, "raw", "(j p) k -> p j k", pieces)
-
+        load_activations("hx", hx, raw_pool, 2)
         load_xg("g", 0)
-        raws["hx"] = load_rows(hx, raw_pool, "raw", "(p j) k -> p j k", 2)
-        load_xg("g", 1)
-        load_weight(("w", "g", 0), 2)
-        load_xg("f", 0)
-        load_weight(("w", "g", 1))
-        raws["cx"] = load_rows(cx, const, "cx_raw", "(p j) k -> p j k", 1)
-        load_xg("i", 0)
+        load_weights("g", 0)
         load_decay()
-        load_weight(("w", "f", 0))
-        load_weight(("p", "f", 0))
+        load_xg("g", 1)
+        load_weights("g", 1)
+        load_activations("cx", cx, const, 1)
+        load_weights("f", 0)
+        load_xg("f", 0)
+        load_xg("i", 0)
+        load_weights("i", 0)
         load_xg("f", 1)
-        load_weight(("w", "i", 0))
+        load_weights("f", 1)
         load_xg("i", 1)
-        load_weight(("p", "i", 0))
-        load_weight(("w", "f", 1))
-        load_weight(("p", "f", 1))
-        load_weight(("w", "i", 1))
-        load_weight(("p", "i", 1))
+        load_weights("i", 1)
+        load_weights("f", 2)
+        load_weights("i", 2)
+        load_weights("f", 3)
+        load_weights("i", 3)
 
         flipped = {}
         grouped = {}
@@ -160,107 +166,98 @@ def tile_ircnn_lstmcell_pa_kernel(
             quantised[key] = (codes, scales)
 
         def spread_bias(gate, half, pool, tag):
-            bank = pool.tile([P, BLOCK], F32, name="spread", tag=tag)
+            bank = pool.tile([P, 2 * QUARTER], F32, name="spread", tag=tag)
             nc.tensor.matmul(
                 out=bank[:],
                 lhsT=ones[:],
-                rhs=bias_rows[gate][:, half * BLOCK : (half + 1) * BLOCK],
+                rhs=bias_rows[gate][:, half * 2 * QUARTER : (half + 1) * 2 * QUARTER],
                 start=True,
                 stop=True,
             )
             spreads[gate, half] = bank
 
-        def add_bias(gate, half, pairs):
-            if (gate, half) not in pre:
-                pre[gate, half] = gate_pool.tile(
-                    [P, BATCH_TILES, BLOCK], F32, name="pre_%s%d" % (gate, half)
+        def keep_bias(gate, half):
+            spread_bias(gate, half, flip_psum, "flip")
+            kept = const.tile([P, 2 * QUARTER], BF16, name="bias_%s%d" % (gate, half))
+            nc.scalar.copy(out=kept[:], in_=spreads[gate, half][:])
+            spreads[gate, half] = kept
+
+        def add_bias(engine, gate, number, pairs):
+            if (gate, number) not in pre:
+                pre[gate, number] = gate_pool.tile(
+                    [P, BATCH_TILES, QUARTER], F32, name="pre_%s%d" % (gate, number)
                 )
+            half, odd = divmod(number, 2)
+            cols = slice(odd * QUARTER, (odd + 1) * QUARTER)
             for pair in pairs:
                 rows = slice(2 * pair, 2 * pair + 2)
-                nc.vector.tensor_tensor(
-                    out=pre[gate, half][:, rows, :],
-                    in0=xg_parts[gate, half][:, rows, :],
-                    in1=spreads[gate, half][:].unsqueeze(1).to_broadcast([P, 2, BLOCK]),
+                engine.tensor_tensor(
+                    out=pre[gate, number][:, rows, :],
+                    in0=xg_parts[gate, half][:, rows, cols],
+                    in1=spreads[gate, half][:, cols].unsqueeze(1).to_broadcast([P, 2, QUARTER]),
                     op=ALU.add,
                 )
 
-        def multiply(kind, gate, half):
-            act_codes, act_scales = quantised["hx" if kind == "w" else "cx"]
-            w_codes, w_scales = quantised[kind, gate, half]
-            opens = kind == "w"
-            closes = kind == "p" or gate == "g"
-            for t in range(BATCH_TILES):
-                if opens:
-                    accs[gate, half, t] = acc_psum.tile([P, BLOCK], F32, name="acc", tag="acc")
-                batch = slice(t * P, (t + 1) * P)
-                for g in range(PASSES):
-                    nc.tensor.matmul_mx(
-                        out=accs[gate, half, t][:],
-                        lhsT=act_codes[:, g, batch].bitcast(FP8X4),
-                        lhsT_scale=act_scales[:, g, batch],
-                        rhs=w_codes[:, g, :].bitcast(FP8X4),
-                        rhs_scale=w_scales[:, g, :],
-                        start=(opens and g == 0),
-                        stop=(closes and g == PASSES - 1),
-                    )
+        def multiply(gate, number):
+            codes, scales = quantised[gate, number]
+            if gate == "g":
+                units = [(2 * number + n, [("hx", n)]) for n in range(2)]
+            else:
+                units = [(number, [("hx", 0), ("cx", 1)])]
+            for unit, operands in units:
+                passes = [(source, n, g) for source, n in operands for g in range(PASSES)]
+                for pair in range(2):
+                    bank = acc_psum.tile([P, 2, QUARTER], F32, name="acc", tag="acc")
+                    accs[gate, unit, pair] = bank
+                    for slot in range(2):
+                        t = 2 * pair + slot
+                        batch = slice(t * P, (t + 1) * P)
+                        for position, (source, n, g) in enumerate(passes):
+                            act_codes, act_scales = quantised[source]
+                            cols = slice(n * QUARTER, (n + 1) * QUARTER)
+                            nc.tensor.matmul_mx(
+                                out=bank[:, slot, :],
+                                lhsT=act_codes[:, g, batch].bitcast(FP8X4),
+                                lhsT_scale=act_scales[:, g, batch],
+                                rhs=codes[:, g, cols].bitcast(FP8X4),
+                                rhs_scale=scales[:, g, cols],
+                                start=(position == 0),
+                                stop=(position == len(passes) - 1),
+                            )
 
-        def finish_gate(gate, half):
+        def finish_gate(gate, number, pairs):
             func = ACT.Tanh if gate == "g" else ACT.Sigmoid
-            tile = pre[gate, half]
-            for t in range(BATCH_TILES):
+            tile = pre[gate, number]
+            for pair in pairs:
+                part = tile[:, 2 * pair : 2 * pair + 2, :]
                 nc.vector.tensor_tensor(
-                    out=tile[:, t, :], in0=accs[gate, half, t][:], in1=tile[:, t, :], op=ALU.add
+                    out=part, in0=accs[gate, number, pair][:], in1=part, op=ALU.add
                 )
-                nc.scalar.activation(out=tile[:, t, :], in_=tile[:, t, :], func=func)
+                nc.scalar.activation(out=part, in_=part, func=func)
 
-        def scale_f(half):
-            tile = pre["f", half]
-            for t in range(BATCH_TILES):
-                nc.vector.scalar_tensor_tensor(
-                    out=tile[:, t, :], in0=tile[:, t, :], scalar=decay[:, 0, t : t + 1],
-                    in1=raws["cx"][:, t, half * BLOCK : (half + 1) * BLOCK],
-                    op0=ALU.mult, op1=ALU.mult,
-                )
-
-        def scale_i(half, tiles):
-            tile = pre["i", half]
+        def scale_gate(gate, number, tiles):
+            tile = pre[gate, number]
             for t in tiles:
+                if gate == "f":
+                    row, other = 0, raws["cx"][:, t, number * QUARTER : (number + 1) * QUARTER]
+                else:
+                    row, other = 1, pre["g", number][:, t, :]
                 nc.vector.scalar_tensor_tensor(
-                    out=tile[:, t, :], in0=tile[:, t, :], scalar=decay[:, 1, t : t + 1],
-                    in1=pre["g", half][:, t, :], op0=ALU.mult, op1=ALU.mult,
+                    out=tile[:, t, :], in0=tile[:, t, :], scalar=decay[:, row, t : t + 1],
+                    in1=other, op0=ALU.mult, op1=ALU.mult,
                 )
 
         out_rows = out.rearrange("(p t) c -> p t c", p=P)
 
-        def add_and_store(half, tiles):
-            tile = pre["i", half]
-            for t in tiles:
-                nc.vector.tensor_tensor(
-                    out=tile[:, t, :], in0=tile[:, t, :], in1=pre["f", half][:, t, :], op=ALU.add
+        def add_and_store(engine, number, pairs):
+            for pair in pairs:
+                rows = slice(2 * pair, 2 * pair + 2)
+                part = pre["i", number][:, rows, :]
+                engine.tensor_tensor(
+                    out=part, in0=part, in1=pre["f", number][:, rows, :], op=ALU.add
                 )
                 nc.sync.dma_start(
-                    out=out_rows[:, t, half * BLOCK : (half + 1) * BLOCK], in_=tile[:, t, :]
-                )
-
-        def take_in(key):
-            transpose_block(key)
-            group_block(key)
-
-        def keep_bias(gate, half):
-            spread_bias(gate, half, flip_psum, "flip")
-            kept = const.tile([P, BLOCK], BF16, name="bias_%s%d" % (gate, half))
-            nc.scalar.copy(out=kept[:], in_=spreads[gate, half][:])
-            spreads[gate, half] = kept
-
-        def add_bias_aside(gate, half, tiles):
-            if (gate, half) not in pre:
-                pre[gate, half] = gate_pool.tile(
-                    [P, BATCH_TILES, BLOCK], F32, name="pre_%s%d" % (gate, half)
-                )
-            for t in tiles:
-                nc.gpsimd.tensor_tensor(
-                    out=pre[gate, half][:, t, :], in0=xg_parts[gate, half][:, t, :],
-                    in1=spreads[gate, half][:], op=ALU.add,
+                    out=out_rows[:, rows, number * QUARTER : (number + 1) * QUARTER], in_=part
                 )
 
         def make_decay():
@@ -270,85 +267,109 @@ def tile_ircnn_lstmcell_pa_kernel(
                 out=decay[:], in_=td[:, :, 0:BATCH_TILES], func=ACT.Exp, scale=minus_b[:, 0:1]
             )
 
-        decay = const.tile([P, 2, BATCH_TILES], F32, name="decay")
         spread_bias("g", 0, acc_psum, "acc")
         spread_bias("g", 1, acc_psum, "acc")
-        spread_bias("f", 0, acc_psum, "acc")
-        spread_bias("i", 0, acc_psum, "acc")
+        keep_bias("f", 0)
+        keep_bias("i", 0)
         keep_bias("f", 1)
         keep_bias("i", 1)
 
-        add_bias("g", 0, (0, 1))
-        take_in("hx")
-        add_bias("g", 1, (0, 1))
+        add_bias(nc.vector, "g", 0, range(2))
+        transpose_block("hx")
+        group_block("hx")
         quantise_block("hx")
-        take_in(("w", "g", 0))
-        quantise_block(("w", "g", 0))
-
-        take_in(("w", "g", 1))
-        add_bias("f", 0, (0, 1))
-
-        multiply("w", "g", 0)
-        take_in("cx")
-        quantise_block(("w", "g", 1))
-        finish_gate("g", 0)
-
-        take_in(("w", "f", 0))
-        quantise_block("cx")
-        add_bias("i", 0, (0,))
-        multiply("w", "g", 1)
-        finish_gate("g", 1)
-
-        take_in(("p", "f", 0))
-        quantise_block(("w", "f", 0))
-        add_bias("i", 0, (1,))
-        add_bias("f", 1, (0,))
+        add_bias(nc.vector, "g", 1, range(2))
+        transpose_block(("g", 0))
+        group_block(("g", 0))
         make_decay()
-
-        take_in(("w", "i", 0))
-        nc.scalar.activation(out=warm[:], in_=warm[:], func=ACT.Sigmoid)
-        quantise_block(("p", "f", 0))
-        add_bias("f", 1, (1,))
-        multiply("w", "f", 0)
+        quantise_block(("g", 0))
         nc.vector.tensor_scalar_mul(out=decay[:], in0=decay[:], scalar1=a_bf[:, 0:1])
 
-        take_in(("p", "i", 0))
-        quantise_block(("w", "i", 0))
-        multiply("p", "f", 0)
-        add_bias("i", 1, (0,))
-        finish_gate("f", 0)
+        transpose_block(("g", 1))
+        group_block(("g", 1))
+        multiply("g", 0)
+        add_bias(nc.vector, "g", 2, range(2))
+        add_bias(nc.vector, "g", 3, range(2))
+        quantise_block(("g", 1))
 
-        take_in(("w", "f", 1))
-        quantise_block(("p", "i", 0))
-        scale_f(0)
-        multiply("w", "i", 0)
+        transpose_block("cx")
+        group_block("cx")
+        transpose_block(("f", 0))
+        group_block(("f", 0))
+        finish_gate("g", 0, range(2))
+        finish_gate("g", 1, range(2))
+        multiply("g", 1)
+        add_bias(nc.vector, "f", 0, range(2))
+        quantise_block("cx")
+        add_bias(nc.vector, "f", 1, range(2))
+        quantise_block(("f", 0))
 
-        take_in(("p", "f", 1))
-        quantise_block(("w", "f", 1))
-        add_bias("i", 1, (1,))
-        multiply("p", "i", 0)
-        finish_gate("i", 0)
+        transpose_block(("i", 0))
+        group_block(("i", 0))
+        finish_gate("g", 2, range(2))
+        finish_gate("g", 3, range(2))
 
-        take_in(("w", "i", 1))
-        quantise_block(("p", "f", 1))
-        scale_i(0, range(BATCH_TILES))
-        multiply("w", "f", 1)
+        multiply("f", 0)
+        add_bias(nc.vector, "i", 0, range(2))
+        quantise_block(("i", 0))
+        add_bias(nc.vector, "i", 1, range(2))
+        transpose_block(("f", 1))
+        group_block(("f", 1))
+        add_bias(nc.vector, "f", 2, range(2))
+        finish_gate("f", 0, range(2))
+        nc.scalar.activation(out=warm[:], in_=warm[:], func=ACT.Sigmoid)
 
-        take_in(("p", "i", 1))
-        quantise_block(("w", "i", 1))
-        add_and_store(0, (0, 1,))
-        multiply("p", "f", 1)
-        finish_gate("f", 1)
+        multiply("i", 0)
+        quantise_block(("f", 1))
+        transpose_block(("i", 1))
+        group_block(("i", 1))
+        add_bias(nc.vector, "f", 3, range(2))
+        scale_gate("f", 0, range(4))
+        finish_gate("i", 0, range(2))
 
-        quantise_block(("p", "i", 1))
-        add_and_store(0, (2, 3,))
-        scale_f(1)
-        multiply("w", "i", 1)
-        multiply("p", "i", 1)
-        finish_gate("i", 1)
-        scale_i(1, (0, 1,))
-        add_and_store(1, (0,))
-        scale_i(1, (2,))
-        add_and_store(1, (1,))
-        scale_i(1, (3,))
-        add_and_store(1, (2, 3,))
+        multiply("f", 1)
+        quantise_block(("i", 1))
+        transpose_block(("f", 2))
+        group_block(("f", 2))
+        add_bias(nc.vector, "i", 2, range(2))
+        scale_gate("i", 0, range(4))
+        finish_gate("f", 1, range(2))
+
+        multiply("i", 1)
+        quantise_block(("f", 2))
+        transpose_block(("i", 2))
+        group_block(("i", 2))
+        add_bias(nc.vector, "i", 3, range(2))
+        scale_gate("f", 1, range(4))
+        finish_gate("i", 1, range(2))
+
+        multiply("f", 2)
+        quantise_block(("i", 2))
+        transpose_block(("f", 3))
+        group_block(("f", 3))
+        add_and_store(nc.vector, 0, range(2))
+        scale_gate("i", 1, range(4))
+        finish_gate("f", 2, range(2))
+
+        multiply("i", 2)
+        quantise_block(("f", 3))
+        transpose_block(("i", 3))
+        group_block(("i", 3))
+        add_and_store(nc.vector, 1, range(2))
+        scale_gate("f", 2, range(4))
+        finish_gate("i", 2, range(2))
+
+        multiply("f", 3)
+        quantise_block(("i", 3))
+        scale_gate("i", 2, range(4))
+        finish_gate("f", 3, range(2))
+
+        multiply("i", 3)
+        add_and_store(nc.vector, 2, range(2))
+        scale_gate("f", 3, range(4))
+        finish_gate("i", 3, (0,))
+        scale_gate("i", 3, (0, 1,))
+        finish_gate("i", 3, (1,))
+        add_and_store(nc.vector, 3, (0,))
+        scale_gate("i", 3, (2, 3,))
+        add_and_store(nc.vector, 3, (1,))

@@ -43,13 +43,12 @@ def tile_ircnn_lstmcell_pa_kernel(
         ctx.enter_context(tc.manual_schedule())
 
         bias_rows = {}
+        bias_tiles = {}
         for gates, first, engine in (("g", 2 * OUT, nc.vector), ("if", 0, nc.gpsimd)):
             width = OUT * len(gates)
             row = const.tile([P, width], BF16, name="bias_rows_" + gates)
             engine.memset(row[:].bitcast(I32), 0)
-            nc.sync.dma_start(
-                out=row[0:1, :], in_=b_hh[first : first + width].rearrange("(o c) -> o c", o=1)
-            )
+            bias_tiles[gates] = row
             for position, gate in enumerate(gates):
                 bias_rows[gate] = row[:, position * OUT : (position + 1) * OUT]
         ident = const.tile([P, P], F32, name="ident")
@@ -63,6 +62,13 @@ def tile_ircnn_lstmcell_pa_kernel(
         a_bf = const.tile([P, 1], BF16, name="a_bf")
         td = const.tile([P, 2, 16], BF16, name="td")
         decay = const.tile([P, 2, BATCH_TILES], F32, name="decay")
+
+        def load_bias(gates, first):
+            row = bias_tiles[gates]
+            nc.sync.dma_start(
+                out=row[0:1, :],
+                in_=b_hh[first : first + OUT * len(gates)].rearrange("(o c) -> o c", o=1),
+            )
 
         def load_decay():
             nc.sync.dma_start(out=b_bf[:], in_=b.partition_broadcast(P))
@@ -109,6 +115,8 @@ def tile_ircnn_lstmcell_pa_kernel(
             xg_parts[gate, half] = part
 
         load_activations("hx", hx, raw_pool, 2)
+        load_bias("g", 2 * OUT)
+        load_bias("if", 0)
         load_xg("g", 0)
         load_weights("g", 0)
         load_decay()
@@ -267,20 +275,19 @@ def tile_ircnn_lstmcell_pa_kernel(
                 out=decay[:], in_=td[:, :, 0:BATCH_TILES], func=ACT.Exp, scale=minus_b[:, 0:1]
             )
 
-        spread_bias("g", 0, acc_psum, "acc")
-        spread_bias("g", 1, acc_psum, "acc")
-        keep_bias("f", 0)
-        keep_bias("i", 0)
-        keep_bias("f", 1)
-        keep_bias("i", 1)
-
-        add_bias(nc.vector, "g", 0, range(2))
         transpose_block("hx")
         group_block("hx")
+        spread_bias("g", 0, acc_psum, "acc")
+        spread_bias("g", 1, acc_psum, "acc")
+        add_bias(nc.vector, "g", 0, range(2))
         quantise_block("hx")
         add_bias(nc.vector, "g", 1, range(2))
         transpose_block(("g", 0))
         group_block(("g", 0))
+        keep_bias("f", 0)
+        keep_bias("i", 0)
+        keep_bias("f", 1)
+        keep_bias("i", 1)
         make_decay()
         quantise_block(("g", 0))
         nc.vector.tensor_scalar_mul(out=decay[:], in0=decay[:], scalar1=a_bf[:, 0:1])
@@ -362,14 +369,13 @@ def tile_ircnn_lstmcell_pa_kernel(
         multiply("f", 3)
         quantise_block(("i", 3))
         scale_gate("i", 2, range(4))
-        finish_gate("f", 3, range(2))
 
         multiply("i", 3)
+        finish_gate("f", 3, range(2))
+        finish_gate("i", 3, range(2))
         add_and_store(nc.vector, 2, range(2))
         scale_gate("f", 3, range(4))
-        finish_gate("i", 3, (0,))
         scale_gate("i", 3, (0, 1,))
-        finish_gate("i", 3, (1,))
-        add_and_store(nc.vector, 3, (0,))
         scale_gate("i", 3, (2, 3,))
+        add_and_store(nc.vector, 3, (0,))
         add_and_store(nc.vector, 3, (1,))

@@ -290,7 +290,6 @@ def tile_ircnn_lstmcell_pa_kernel(
         keep_bias("i", 1)
         make_decay()
         quantise_block(("g", 0))
-        nc.vector.tensor_scalar_mul(out=decay[:], in0=decay[:], scalar1=a_bf[:, 0:1])
 
         transpose_block(("g", 1))
         group_block(("g", 1))
@@ -298,6 +297,7 @@ def tile_ircnn_lstmcell_pa_kernel(
         add_bias(nc.vector, "g", 2, range(2))
         add_bias(nc.vector, "g", 3, range(2))
         quantise_block(("g", 1))
+        nc.vector.tensor_scalar_mul(out=decay[:], in0=decay[:], scalar1=a_bf[:, 0:1])
 
         transpose_block("cx")
         group_block("cx")
@@ -322,7 +322,7 @@ def tile_ircnn_lstmcell_pa_kernel(
         add_bias(nc.vector, "i", 1, range(2))
         transpose_block(("f", 1))
         group_block(("f", 1))
-        add_bias(nc.vector, "f", 2, range(2))
+        add_bias(nc.gpsimd, "f", 2, range(2))
         finish_gate("f", 0, range(2))
         nc.scalar.activation(out=warm[:], in_=warm[:], func=ACT.Sigmoid)
 
@@ -330,7 +330,7 @@ def tile_ircnn_lstmcell_pa_kernel(
         quantise_block(("f", 1))
         transpose_block(("i", 1))
         group_block(("i", 1))
-        add_bias(nc.vector, "f", 3, range(2))
+        add_bias(nc.gpsimd, "f", 3, range(2))
         scale_gate("f", 0, range(4))
         finish_gate("i", 0, range(2))
 
@@ -338,7 +338,7 @@ def tile_ircnn_lstmcell_pa_kernel(
         quantise_block(("i", 1))
         transpose_block(("f", 2))
         group_block(("f", 2))
-        add_bias(nc.vector, "i", 2, range(2))
+        add_bias(nc.gpsimd, "i", 2, range(2))
         scale_gate("i", 0, range(4))
         finish_gate("f", 1, range(2))
 
@@ -346,7 +346,7 @@ def tile_ircnn_lstmcell_pa_kernel(
         quantise_block(("f", 2))
         transpose_block(("i", 2))
         group_block(("i", 2))
-        add_bias(nc.vector, "i", 3, range(2))
+        add_bias(nc.gpsimd, "i", 3, range(2))
         scale_gate("f", 1, range(4))
         finish_gate("i", 1, range(2))
 
@@ -354,7 +354,7 @@ def tile_ircnn_lstmcell_pa_kernel(
         quantise_block(("i", 2))
         transpose_block(("f", 3))
         group_block(("f", 3))
-        add_and_store(nc.vector, 0, range(2))
+        add_and_store(nc.gpsimd, 0, range(2))
         scale_gate("i", 1, range(4))
         finish_gate("f", 2, range(2))
 
@@ -362,7 +362,7 @@ def tile_ircnn_lstmcell_pa_kernel(
         quantise_block(("f", 3))
         transpose_block(("i", 3))
         group_block(("i", 3))
-        add_and_store(nc.vector, 1, range(2))
+        add_and_store(nc.gpsimd, 1, range(2))
         scale_gate("f", 2, range(4))
         finish_gate("i", 2, range(2))
 

@@ -116,15 +116,15 @@ def tile_ircnn_lstmcell_pa_kernel(
 
         load_activations("hx", hx, raw_pool, 2)
         load_bias("g", 2 * OUT)
-        load_bias("if", 0)
         load_xg("g", 0)
         load_weights("g", 0)
+        load_bias("if", 0)
         load_decay()
         load_xg("g", 1)
         load_weights("g", 1)
+        load_xg("f", 0)
         load_activations("cx", cx, const, 1)
         load_weights("f", 0)
-        load_xg("f", 0)
         load_xg("i", 0)
         load_weights("i", 0)
         load_xg("f", 1)
@@ -298,6 +298,7 @@ def tile_ircnn_lstmcell_pa_kernel(
         add_bias(nc.vector, "g", 3, range(2))
         quantise_block(("g", 1))
         nc.vector.tensor_scalar_mul(out=decay[:], in0=decay[:], scalar1=a_bf[:, 0:1])
+        add_bias(nc.gpsimd, "f", 0, range(2))
 
         transpose_block("cx")
         group_block("cx")
@@ -306,9 +307,8 @@ def tile_ircnn_lstmcell_pa_kernel(
         finish_gate("g", 0, range(2))
         finish_gate("g", 1, range(2))
         multiply("g", 1)
-        add_bias(nc.vector, "f", 0, range(2))
         quantise_block("cx")
-        add_bias(nc.vector, "f", 1, range(2))
+        add_bias(nc.gpsimd, "f", 1, range(2))
         quantise_block(("f", 0))
 
         transpose_block(("i", 0))
@@ -319,10 +319,10 @@ def tile_ircnn_lstmcell_pa_kernel(
         multiply("f", 0)
         add_bias(nc.vector, "i", 0, range(2))
         quantise_block(("i", 0))
-        add_bias(nc.vector, "i", 1, range(2))
+        add_bias(nc.gpsimd, "i", 1, range(2))
         transpose_block(("f", 1))
         group_block(("f", 1))
-        add_bias(nc.gpsimd, "f", 2, range(2))
+        add_bias(nc.vector, "f", 2, range(2))
         finish_gate("f", 0, range(2))
         nc.scalar.activation(out=warm[:], in_=warm[:], func=ACT.Sigmoid)
 
@@ -330,7 +330,7 @@ def tile_ircnn_lstmcell_pa_kernel(
         quantise_block(("f", 1))
         transpose_block(("i", 1))
         group_block(("i", 1))
-        add_bias(nc.gpsimd, "f", 3, range(2))
+        add_bias(nc.vector, "f", 3, range(2))
         scale_gate("f", 0, range(4))
         finish_gate("i", 0, range(2))
 

@@ -25,6 +25,8 @@ BATCH_TILES = B // P
 WORDS = K // 2
 GATE_COLUMN = {"i": 0, "f": OUT, "g": 2 * OUT}
 
+LOG2_E = 1.4426950408889634
+
 FLOPS = 2 * B * K * (3 * OUT + 2 * OUT)
 
 
@@ -57,7 +59,9 @@ def tile_ircnn_lstmcell_pa_kernel(
         nc.vector.memset(ones[:], 1.0)
         warm = const.tile([P, 1], F32, name="warm")
         nc.vector.memset(warm[:], 0.0)
-        nc.scalar.activation(out=warm[:], in_=warm[:], func=ACT.Exp)
+        nc.scalar.activation(out=warm[:], in_=warm[:], func=ACT.Sigmoid)
+        twos = const.tile([P, 2, BATCH_TILES], F32, name="twos")
+        nc.vector.memset(twos[:], 2.0)
         b_bf = const.tile([P, 1], BF16, name="b_bf")
         a_bf = const.tile([P, 1], BF16, name="a_bf")
         td = const.tile([P, 2, 16], BF16, name="td")
@@ -99,7 +103,7 @@ def tile_ircnn_lstmcell_pa_kernel(
             for n, (source, first) in enumerate(pieces):
                 nc.sync.dma_start(
                     out=raw[:, 2 * n : 2 * n + 2, :],
-                    in_=source[first : first + QUARTER, :].rearrange("(j p) k -> p j k", p=P),
+                    in_=source[first : first + QUARTER, :].rearrange("(p j) k -> p j k", p=P),
                 )
             raws[gate, number] = raw
 
@@ -185,24 +189,25 @@ def tile_ircnn_lstmcell_pa_kernel(
             spreads[gate, half] = bank
 
         def keep_bias(gate, half):
-            spread_bias(gate, half, flip_psum, "flip")
+            spread_bias(gate, half, acc_psum, "acc")
             kept = const.tile([P, 2 * QUARTER], BF16, name="bias_%s%d" % (gate, half))
             nc.scalar.copy(out=kept[:], in_=spreads[gate, half][:])
             spreads[gate, half] = kept
 
-        def add_bias(engine, gate, number, pairs):
+        def add_bias(engine, gate, number):
             if (gate, number) not in pre:
                 pre[gate, number] = gate_pool.tile(
                     [P, BATCH_TILES, QUARTER], F32, name="pre_%s%d" % (gate, number)
                 )
             half, odd = divmod(number, 2)
             cols = slice(odd * QUARTER, (odd + 1) * QUARTER)
-            for pair in pairs:
-                rows = slice(2 * pair, 2 * pair + 2)
+            step = BATCH_TILES if engine is nc.vector else 2
+            for t in range(0, BATCH_TILES, step):
+                rows = slice(t, t + step)
                 engine.tensor_tensor(
                     out=pre[gate, number][:, rows, :],
                     in0=xg_parts[gate, half][:, rows, cols],
-                    in1=spreads[gate, half][:, cols].unsqueeze(1).to_broadcast([P, 2, QUARTER]),
+                    in1=spreads[gate, half][:, cols].unsqueeze(1).to_broadcast([P, step, QUARTER]),
                     op=ALU.add,
                 )
 
@@ -238,8 +243,12 @@ def tile_ircnn_lstmcell_pa_kernel(
             tile = pre[gate, number]
             for pair in pairs:
                 part = tile[:, 2 * pair : 2 * pair + 2, :]
+                by_row = part.rearrange("b t (p j) -> b t p j", j=2)
                 nc.vector.tensor_tensor(
-                    out=part, in0=accs[gate, number, pair][:], in1=part, op=ALU.add
+                    out=by_row,
+                    in0=accs[gate, number, pair][:].rearrange("b t (j p) -> b t p j", j=2),
+                    in1=by_row,
+                    op=ALU.add,
                 )
                 nc.scalar.activation(out=part, in_=part, func=func)
 
@@ -269,36 +278,39 @@ def tile_ircnn_lstmcell_pa_kernel(
                 )
 
         def make_decay():
-            minus_b = const.tile([P, 1], F32, name="minus_b")
-            nc.vector.tensor_scalar_mul(out=minus_b[:], in0=b_bf[:], scalar1=-1.0)
-            nc.scalar.activation(
-                out=decay[:], in_=td[:, :, 0:BATCH_TILES], func=ACT.Exp, scale=minus_b[:, 0:1]
+            rate = const.tile([P, 1], F32, name="rate")
+            nc.vector.tensor_copy(out=rate[:], in_=b_bf[:])
+            exponent = const.tile([P, 2, BATCH_TILES], F32, name="exponent")
+            nc.vector.tensor_scalar(
+                out=exponent[:], in0=td[:, :, 0:BATCH_TILES], scalar1=rate[:, 0:1], scalar2=-LOG2_E,
+                op0=ALU.mult, op1=ALU.mult,
             )
+            nc.gpsimd.tensor_tensor(out=decay[:], in0=twos[:], in1=exponent[:], op=ALU.pow)
 
         transpose_block("hx")
         group_block("hx")
         spread_bias("g", 0, acc_psum, "acc")
         spread_bias("g", 1, acc_psum, "acc")
-        add_bias(nc.vector, "g", 0, range(2))
+        add_bias(nc.vector, "g", 0)
         quantise_block("hx")
-        add_bias(nc.vector, "g", 1, range(2))
+        add_bias(nc.vector, "g", 1)
         transpose_block(("g", 0))
         group_block(("g", 0))
+        make_decay()
+        quantise_block(("g", 0))
         keep_bias("f", 0)
         keep_bias("i", 0)
         keep_bias("f", 1)
         keep_bias("i", 1)
-        make_decay()
-        quantise_block(("g", 0))
 
         transpose_block(("g", 1))
         group_block(("g", 1))
         multiply("g", 0)
-        add_bias(nc.vector, "g", 2, range(2))
-        add_bias(nc.vector, "g", 3, range(2))
+        add_bias(nc.vector, "g", 2)
+        add_bias(nc.vector, "g", 3)
         quantise_block(("g", 1))
         nc.vector.tensor_scalar_mul(out=decay[:], in0=decay[:], scalar1=a_bf[:, 0:1])
-        add_bias(nc.gpsimd, "f", 0, range(2))
+        add_bias(nc.gpsimd, "f", 0)
 
         transpose_block("cx")
         group_block("cx")
@@ -308,7 +320,7 @@ def tile_ircnn_lstmcell_pa_kernel(
         finish_gate("g", 1, range(2))
         multiply("g", 1)
         quantise_block("cx")
-        add_bias(nc.gpsimd, "f", 1, range(2))
+        add_bias(nc.gpsimd, "f", 1)
         quantise_block(("f", 0))
 
         transpose_block(("i", 0))
@@ -317,20 +329,19 @@ def tile_ircnn_lstmcell_pa_kernel(
         finish_gate("g", 3, range(2))
 
         multiply("f", 0)
-        add_bias(nc.vector, "i", 0, range(2))
+        add_bias(nc.vector, "i", 0)
         quantise_block(("i", 0))
-        add_bias(nc.gpsimd, "i", 1, range(2))
+        add_bias(nc.gpsimd, "i", 1)
         transpose_block(("f", 1))
         group_block(("f", 1))
-        add_bias(nc.vector, "f", 2, range(2))
+        add_bias(nc.vector, "f", 2)
         finish_gate("f", 0, range(2))
-        nc.scalar.activation(out=warm[:], in_=warm[:], func=ACT.Sigmoid)
 
         multiply("i", 0)
         quantise_block(("f", 1))
         transpose_block(("i", 1))
         group_block(("i", 1))
-        add_bias(nc.vector, "f", 3, range(2))
+        add_bias(nc.vector, "f", 3)
         scale_gate("f", 0, range(4))
         finish_gate("i", 0, range(2))
 
@@ -338,7 +349,7 @@ def tile_ircnn_lstmcell_pa_kernel(
         quantise_block(("i", 1))
         transpose_block(("f", 2))
         group_block(("f", 2))
-        add_bias(nc.gpsimd, "i", 2, range(2))
+        add_bias(nc.gpsimd, "i", 2)
         scale_gate("i", 0, range(4))
         finish_gate("f", 1, range(2))
 
@@ -346,7 +357,7 @@ def tile_ircnn_lstmcell_pa_kernel(
         quantise_block(("f", 2))
         transpose_block(("i", 2))
         group_block(("i", 2))
-        add_bias(nc.gpsimd, "i", 3, range(2))
+        add_bias(nc.gpsimd, "i", 3)
         scale_gate("f", 1, range(4))
         finish_gate("i", 1, range(2))
 

@@ -194,15 +194,21 @@ def tile_ircnn_lstmcell_pa_kernel(
             nc.scalar.copy(out=kept[:], in_=spreads[gate, half][:])
             spreads[gate, half] = kept
 
-        def add_bias(engine, gate, number):
+        def new_pre(gate, number):
+            if (gate, number) not in pre:
+                pre[gate, number] = gate_pool.tile(
+                    [P, BATCH_TILES, QUARTER], F32, name="pre_%s%d" % (gate, number)
+                )
+
+        def add_bias(engine, gate, number, pairs=None):
             if (gate, number) not in pre:
                 pre[gate, number] = gate_pool.tile(
                     [P, BATCH_TILES, QUARTER], F32, name="pre_%s%d" % (gate, number)
                 )
             half, odd = divmod(number, 2)
             cols = slice(odd * QUARTER, (odd + 1) * QUARTER)
-            step = BATCH_TILES if engine is nc.vector else 2
-            for t in range(0, BATCH_TILES, step):
+            step = BATCH_TILES if pairs is None else 2
+            for t in range(0, BATCH_TILES, step) if pairs is None else [2 * pair for pair in pairs]:
                 rows = slice(t, t + step)
                 engine.tensor_tensor(
                     out=pre[gate, number][:, rows, :],
@@ -310,7 +316,7 @@ def tile_ircnn_lstmcell_pa_kernel(
         add_bias(nc.vector, "g", 3)
         quantise_block(("g", 1))
         nc.vector.tensor_scalar_mul(out=decay[:], in0=decay[:], scalar1=a_bf[:, 0:1])
-        add_bias(nc.gpsimd, "f", 0)
+        add_bias(nc.vector, "f", 0)
 
         transpose_block("cx")
         group_block("cx")
@@ -320,7 +326,7 @@ def tile_ircnn_lstmcell_pa_kernel(
         finish_gate("g", 1, range(2))
         multiply("g", 1)
         quantise_block("cx")
-        add_bias(nc.gpsimd, "f", 1)
+        add_bias(nc.gpsimd, "f", 1, (0, 1))
         quantise_block(("f", 0))
 
         transpose_block(("i", 0))
@@ -331,7 +337,7 @@ def tile_ircnn_lstmcell_pa_kernel(
         multiply("f", 0)
         add_bias(nc.vector, "i", 0)
         quantise_block(("i", 0))
-        add_bias(nc.gpsimd, "i", 1)
+        add_bias(nc.gpsimd, "i", 1, (0, 1))
         transpose_block(("f", 1))
         group_block(("f", 1))
         add_bias(nc.vector, "f", 2)
@@ -341,7 +347,7 @@ def tile_ircnn_lstmcell_pa_kernel(
         quantise_block(("f", 1))
         transpose_block(("i", 1))
         group_block(("i", 1))
-        add_bias(nc.vector, "f", 3)
+        add_bias(nc.gpsimd, "f", 3, (0, 1))
         scale_gate("f", 0, range(4))
         finish_gate("i", 0, range(2))
 
@@ -349,7 +355,7 @@ def tile_ircnn_lstmcell_pa_kernel(
         quantise_block(("i", 1))
         transpose_block(("f", 2))
         group_block(("f", 2))
-        add_bias(nc.gpsimd, "i", 2)
+        add_bias(nc.vector, "i", 2)
         scale_gate("i", 0, range(4))
         finish_gate("f", 1, range(2))
 
@@ -357,7 +363,7 @@ def tile_ircnn_lstmcell_pa_kernel(
         quantise_block(("f", 2))
         transpose_block(("i", 2))
         group_block(("i", 2))
-        add_bias(nc.gpsimd, "i", 3)
+        add_bias(nc.gpsimd, "i", 3, (0, 1))
         scale_gate("f", 1, range(4))
         finish_gate("i", 1, range(2))
 

@@ -157,7 +157,7 @@ def tile_ircnn_lstmcell_pa_kernel(
                 flipped[key, j] = bank
 
         def group_block(key):
-            tile = grouped_pool.tile([P, PASSES * BLOCK * 4], BF16, name="grouped", align_bytes=64)
+            tile = grouped_pool.tile([P, PASSES * BLOCK * 4], BF16, name="grouped", align_bytes=256)
             target = tile[:].bitcast(F32).rearrange("p (g r u) -> p g r u", g=PASSES, u=2)
             for j in range(ROW_TILES):
                 nc.scalar.copy(
@@ -168,8 +168,8 @@ def tile_ircnn_lstmcell_pa_kernel(
 
         def quantise_block(key):
             pool, name = (const, key) if key in ("hx", "cx") else (weight_pool, "w")
-            codes = pool.tile([P, PASSES, BLOCK], U32, name=name + "_codes", align_bytes=64)
-            scales = pool.tile([P, PASSES, BLOCK], U8, name=name + "_scales", align_bytes=64)
+            codes = pool.tile([P, PASSES, BLOCK], U32, name=name + "_codes", align_bytes=256)
+            scales = pool.tile([P, PASSES, BLOCK], U8, name=name + "_scales", align_bytes=256)
             nc.vector.quantize_mx(
                 out=codes[:].rearrange("p g r -> p (g r)").bitcast(FP8X4),
                 scales=scales[:].rearrange("p g r -> p (g r)"),
@@ -283,6 +283,21 @@ def tile_ircnn_lstmcell_pa_kernel(
                     out=out_rows[:, rows, number * QUARTER : (number + 1) * QUARTER], in_=part
                 )
 
+        def sum_by_matmul(number, pairs):
+            for pair in pairs:
+                rows = slice(2 * pair, 2 * pair + 2)
+                part = pre["i", number][:, rows, :]
+                bank = acc_psum.tile([P, 2, QUARTER], F32, name="total", tag="acc")
+                for term, last in ((part, False), (pre["f", number][:, rows, :], True)):
+                    nc.tensor.matmul(
+                        out=bank[:].rearrange("b t c -> b (t c)"), lhsT=ident[:],
+                        rhs=term.rearrange("b t c -> b (t c)"), start=not last, stop=last,
+                    )
+                nc.scalar.copy(out=part, in_=bank[:])
+                nc.sync.dma_start(
+                    out=out_rows[:, rows, number * QUARTER : (number + 1) * QUARTER], in_=part
+                )
+
         def make_decay():
             rate = const.tile([P, 1], F32, name="rate")
             nc.vector.tensor_copy(out=rate[:], in_=b_bf[:])
@@ -390,7 +405,8 @@ def tile_ircnn_lstmcell_pa_kernel(
         multiply("i", 3)
         finish_gate("f", 3, range(2))
         finish_gate("i", 3, range(2))
-        add_and_store(nc.vector, 2, range(2))
+        sum_by_matmul(2, (0,))
+        add_and_store(nc.vector, 2, (1,))
         scale_gate("f", 3, range(4))
         scale_gate("i", 3, (0, 1,))
         scale_gate("i", 3, (2, 3,))

@@ -47,7 +47,7 @@ def tile_ircnn_lstmcell_pa_kernel(
         bias_rows = {}
         bias_tiles = {}
         for gates, first, engine in (("g", 2 * OUT, nc.vector), ("if", 0, nc.gpsimd)):
-            width = OUT * len(gates)
+            width = OUT * len(gates) + (48 if gates == "g" else 0)
             row = const.tile([P, width], BF16, name="bias_rows_" + gates)
             engine.memset(row[:].bitcast(I32), 0)
             bias_tiles[gates] = row
@@ -62,21 +62,21 @@ def tile_ircnn_lstmcell_pa_kernel(
         nc.scalar.activation(out=warm[:], in_=warm[:], func=ACT.Sigmoid)
         twos = const.tile([P, 2, BATCH_TILES], F32, name="twos")
         nc.vector.memset(twos[:], 2.0)
-        b_bf = const.tile([P, 1], BF16, name="b_bf")
-        a_bf = const.tile([P, 1], BF16, name="a_bf")
+        rate = const.tile([P, 32], F32, name="rate")
         td = const.tile([P, 2, 16], BF16, name="td")
         decay = const.tile([P, 2, BATCH_TILES], F32, name="decay")
 
         def load_bias(gates, first):
             row = bias_tiles[gates]
             nc.sync.dma_start(
-                out=row[0:1, :],
+                out=row[0:1, 0 : OUT * len(gates)],
                 in_=b_hh[first : first + OUT * len(gates)].rearrange("(o c) -> o c", o=1),
             )
 
         def load_decay():
-            nc.sync.dma_start(out=b_bf[:], in_=b.partition_broadcast(P))
-            nc.sync.dma_start(out=a_bf[:], in_=a.partition_broadcast(P))
+            row = bias_tiles["g"]
+            nc.sync.dma_start(out=row[0:1, OUT + 16 : OUT + 17], in_=b.rearrange("(o c) -> o c", o=1))
+            nc.sync.dma_start(out=row[0:1, OUT + 32 : OUT + 33], in_=a.rearrange("(o c) -> o c", o=1))
             nc.sync.dma_start(out=td[:, 0, 0:BATCH_TILES], in_=td0.rearrange("(p t) -> p t", p=P))
             nc.sync.dma_start(out=td[:, 1, 0:BATCH_TILES], in_=td1.rearrange("(p t) -> p t", p=P))
 
@@ -299,8 +299,12 @@ def tile_ircnn_lstmcell_pa_kernel(
                 )
 
         def make_decay():
-            rate = const.tile([P, 1], F32, name="rate")
-            nc.vector.tensor_copy(out=rate[:], in_=b_bf[:])
+            bank = flip_psum.tile([P, 2 * QUARTER], F32, name="rates", tag="flip")
+            nc.tensor.matmul(
+                out=bank[:, 0:32], lhsT=ones[:], rhs=bias_tiles["g"][:, OUT + 16 : OUT + 48],
+                start=True, stop=True,
+            )
+            nc.vector.tensor_copy(out=rate[:], in_=bank[:, 0:32])
             exponent = const.tile([P, 2, BATCH_TILES], F32, name="exponent")
             nc.vector.tensor_scalar(
                 out=exponent[:], in0=td[:, :, 0:BATCH_TILES], scalar1=rate[:, 0:1], scalar2=-LOG2_E,
@@ -330,7 +334,7 @@ def tile_ircnn_lstmcell_pa_kernel(
         add_bias(nc.vector, "g", 2)
         add_bias(nc.vector, "g", 3)
         quantise_block(("g", 1))
-        nc.vector.tensor_scalar_mul(out=decay[:], in0=decay[:], scalar1=a_bf[:, 0:1])
+        nc.vector.tensor_scalar_mul(out=decay[:], in0=decay[:], scalar1=rate[:, 16:17])
         add_bias(nc.vector, "f", 0)
 
         transpose_block("cx")

@@ -90,8 +90,10 @@ def tile_ircnn_lstmcell_pa_kernel(
                 nc.sync.dma_start(out=raw[:, j : j + step, :], in_=rows[:, j : j + step, :])
             raws[key] = raw
 
-        def load_weights(gate, number):
-            raw = raw_pool.tile([P, ROW_TILES, K], BF16, name="raw")
+        def load_weights(gate, number, parts=range(2)):
+            if (gate, number) not in raws:
+                raws[gate, number] = raw_pool.tile([P, ROW_TILES, K], BF16, name="raw")
+            raw = raws[gate, number]
             if gate == "g":
                 pieces = [(w_hh, 2 * OUT + (2 * number + n) * QUARTER) for n in range(2)]
             else:
@@ -100,12 +102,12 @@ def tile_ircnn_lstmcell_pa_kernel(
                     (w_hh, GATE_COLUMN[gate] + number * QUARTER),
                     (peephole, number * QUARTER),
                 ]
-            for n, (source, first) in enumerate(pieces):
+            for n in parts:
+                source, first = pieces[n]
                 nc.sync.dma_start(
                     out=raw[:, 2 * n : 2 * n + 2, :],
                     in_=source[first : first + QUARTER, :].rearrange("(p j) k -> p j k", p=P),
                 )
-            raws[gate, number] = raw
 
         xg_parts = {}
 
@@ -120,8 +122,9 @@ def tile_ircnn_lstmcell_pa_kernel(
 
         load_activations("hx", hx, raw_pool, 2)
         load_bias("g", 2 * OUT)
+        load_weights("g", 0, (0,))
         load_xg("g", 0)
-        load_weights("g", 0)
+        load_weights("g", 0, (1,))
         load_bias("if", 0)
         load_decay()
         load_xg("g", 1)
@@ -147,9 +150,9 @@ def tile_ircnn_lstmcell_pa_kernel(
         pre = {}
         accs = {}
 
-        def transpose_block(key):
+        def transpose_block(key, tiles=range(ROW_TILES)):
             words = raws[key][:].rearrange("p j k -> p (j k)").bitcast(F32)
-            for j in range(ROW_TILES):
+            for j in tiles:
                 bank = flip_psum.tile([P, 2 * PASSES, P], F32, name="flipped", tag="flip")
                 for q in range(2 * PASSES):
                     first = j * WORDS + q * P
@@ -189,7 +192,7 @@ def tile_ircnn_lstmcell_pa_kernel(
             spreads[gate, half] = bank
 
         def keep_bias(gate, half):
-            spread_bias(gate, half, acc_psum, "acc")
+            spread_bias(gate, half, flip_psum, "flip")
             kept = const.tile([P, 2 * QUARTER], BF16, name="bias_%s%d" % (gate, half))
             nc.scalar.copy(out=kept[:], in_=spreads[gate, half][:])
             spreads[gate, half] = kept
@@ -217,7 +220,7 @@ def tile_ircnn_lstmcell_pa_kernel(
                     op=ALU.add,
                 )
 
-        def multiply(gate, number):
+        def multiply(gate, number, pairs=range(2)):
             codes, scales = quantised[gate, number]
             if gate == "g":
                 units = [(2 * number + n, [("hx", n)]) for n in range(2)]
@@ -225,7 +228,7 @@ def tile_ircnn_lstmcell_pa_kernel(
                 units = [(number, [("hx", 0), ("cx", 1)])]
             for unit, operands in units:
                 passes = [(source, n, g) for source, n in operands for g in range(PASSES)]
-                for pair in range(2):
+                for pair in pairs:
                     bank = acc_psum.tile([P, 2, QUARTER], F32, name="acc", tag="acc")
                     accs[gate, unit, pair] = bank
                     for slot in range(2):
@@ -244,8 +247,14 @@ def tile_ircnn_lstmcell_pa_kernel(
                                 stop=(position == len(passes) - 1),
                             )
 
+        def activate(gate, number, pairs=range(2)):
+            for pair in pairs:
+                part = pre[gate, number][:, 2 * pair : 2 * pair + 2, :]
+                nc.scalar.activation(
+                    out=part, in_=part, func=ACT.Tanh if gate == "g" else ACT.Sigmoid
+                )
+
         def finish_gate(gate, number, pairs):
-            func = ACT.Tanh if gate == "g" else ACT.Sigmoid
             tile = pre[gate, number]
             for pair in pairs:
                 part = tile[:, 2 * pair : 2 * pair + 2, :]
@@ -256,7 +265,6 @@ def tile_ircnn_lstmcell_pa_kernel(
                     in1=by_row,
                     op=ALU.add,
                 )
-                nc.scalar.activation(out=part, in_=part, func=func)
 
         def scale_gate(gate, number, tiles):
             tile = pre[gate, number]
@@ -315,11 +323,11 @@ def tile_ircnn_lstmcell_pa_kernel(
         transpose_block("hx")
         group_block("hx")
         spread_bias("g", 0, acc_psum, "acc")
-        spread_bias("g", 1, acc_psum, "acc")
         add_bias(nc.vector, "g", 0)
         quantise_block("hx")
         add_bias(nc.vector, "g", 1)
         transpose_block(("g", 0))
+        spread_bias("g", 1, acc_psum, "acc")
         group_block(("g", 0))
         make_decay()
         quantise_block(("g", 0))
@@ -330,9 +338,9 @@ def tile_ircnn_lstmcell_pa_kernel(
 
         transpose_block(("g", 1))
         group_block(("g", 1))
-        multiply("g", 0)
         add_bias(nc.vector, "g", 2)
         add_bias(nc.vector, "g", 3)
+        multiply("g", 0)
         quantise_block(("g", 1))
         nc.vector.tensor_scalar_mul(out=decay[:], in0=decay[:], scalar1=rate[:, 16:17])
         add_bias(nc.vector, "f", 0)
@@ -342,7 +350,9 @@ def tile_ircnn_lstmcell_pa_kernel(
         transpose_block(("f", 0))
         group_block(("f", 0))
         finish_gate("g", 0, range(2))
+        activate("g", 0)
         finish_gate("g", 1, range(2))
+        activate("g", 1)
         multiply("g", 1)
         quantise_block("cx")
         add_bias(nc.gpsimd, "f", 1, (0, 1))
@@ -351,7 +361,9 @@ def tile_ircnn_lstmcell_pa_kernel(
         transpose_block(("i", 0))
         group_block(("i", 0))
         finish_gate("g", 2, range(2))
+        activate("g", 2)
         finish_gate("g", 3, range(2))
+        activate("g", 3)
 
         multiply("f", 0)
         add_bias(nc.vector, "i", 0)
@@ -361,6 +373,7 @@ def tile_ircnn_lstmcell_pa_kernel(
         group_block(("f", 1))
         add_bias(nc.vector, "f", 2)
         finish_gate("f", 0, range(2))
+        activate("f", 0)
 
         multiply("i", 0)
         quantise_block(("f", 1))
@@ -369,6 +382,7 @@ def tile_ircnn_lstmcell_pa_kernel(
         add_bias(nc.gpsimd, "f", 3, (0, 1))
         scale_gate("f", 0, range(4))
         finish_gate("i", 0, range(2))
+        activate("i", 0)
 
         multiply("f", 1)
         quantise_block(("i", 1))
@@ -377,6 +391,7 @@ def tile_ircnn_lstmcell_pa_kernel(
         add_bias(nc.vector, "i", 2)
         scale_gate("i", 0, range(4))
         finish_gate("f", 1, range(2))
+        activate("f", 1)
 
         multiply("i", 1)
         quantise_block(("f", 2))
@@ -385,6 +400,7 @@ def tile_ircnn_lstmcell_pa_kernel(
         add_bias(nc.gpsimd, "i", 3, (0, 1))
         scale_gate("f", 1, range(4))
         finish_gate("i", 1, range(2))
+        activate("i", 1)
 
         multiply("f", 2)
         quantise_block(("i", 2))
@@ -393,24 +409,30 @@ def tile_ircnn_lstmcell_pa_kernel(
         add_and_store(nc.gpsimd, 0, range(2))
         scale_gate("i", 1, range(4))
         finish_gate("f", 2, range(2))
+        activate("f", 2)
 
-        multiply("i", 2)
+        multiply("i", 2, (0,))
+        transpose_block(("i", 3), (0, 1))
+        multiply("i", 2, (1,))
         quantise_block(("f", 3))
-        transpose_block(("i", 3))
+        transpose_block(("i", 3), (2, 3))
         group_block(("i", 3))
         add_and_store(nc.gpsimd, 1, range(2))
         scale_gate("f", 2, range(4))
         finish_gate("i", 2, range(2))
+        activate("i", 2)
 
         multiply("f", 3)
         quantise_block(("i", 3))
         scale_gate("i", 2, range(4))
+        add_and_store(nc.gpsimd, 2, (1,))
 
         multiply("i", 3)
         finish_gate("f", 3, range(2))
+        activate("f", 3)
         finish_gate("i", 3, range(2))
+        activate("i", 3)
         sum_by_matmul(2, (0,))
-        add_and_store(nc.vector, 2, (1,))
         scale_gate("f", 3, range(4))
         scale_gate("i", 3, (0, 1,))
         scale_gate("i", 3, (2, 3,))

from contextlib import ExitStack

import concourse.mybir as mybir
from concourse.masks import make_identity

F32 = mybir.dt.float32
BF16 = mybir.dt.bfloat16
I32 = mybir.dt.int32
U32 = mybir.dt.uint32
U8 = mybir.dt.uint8
FP8X4 = mybir.dt.float8_e4m3fn_x4
ACT = mybir.ActivationFunctionType
ALU = mybir.AluOpType

P = 128
B = 512
K = 1024
OUT = 1024
K_PASS = 512
PASSES = K // K_PASS
BLOCK = 512
ROW_TILES = BLOCK // P
QUARTER = 256
BATCH_TILES = B // P
WORDS = K // 2
GATE_COLUMN = {"i": 0, "f": OUT, "g": 2 * OUT}

LOG2_E = 1.4426950408889634

FLOPS = 2 * B * K * (3 * OUT + 2 * OUT)


def tile_ircnn_lstmcell_pa_kernel(
    tc, xg, hx, cx, td0, td1, w_hh, w_pi, w_pf, b_hh, a, b, out
):
    nc = tc.nc
    with ExitStack() as ctx:
        const = ctx.enter_context(tc.tile_pool(name="const", bufs=1))
        raw_pool = ctx.enter_context(tc.tile_pool(name="raw", bufs=11))
        grouped_pool = ctx.enter_context(tc.tile_pool(name="grouped", bufs=3))
        weight_pool = ctx.enter_context(tc.tile_pool(name="weight", bufs=3))
        gate_pool = ctx.enter_context(tc.tile_pool(name="gate", bufs=1))
        flip_psum = ctx.enter_context(tc.psum_pool(name="flip", bufs=4))
        acc_psum = ctx.enter_context(tc.psum_pool(name="acc", bufs=4))
        ctx.enter_context(tc.manual_schedule())

        bias_rows = {}
        bias_tiles = {}
        for gates, first, engine in (("g", 2 * OUT, nc.vector), ("if", 0, nc.gpsimd)):
            width = OUT * len(gates) + (48 if gates == "g" else 0)
            row = const.tile([P, width], BF16, name="bias_rows_" + gates)
            engine.memset(row[:].bitcast(I32), 0)
            bias_tiles[gates] = row
            for position, gate in enumerate(gates):
                bias_rows[gate] = row[:, position * OUT : (position + 1) * OUT]
        ident = const.tile([P, P], F32, name="ident")
        make_identity(nc, ident[:])
        ones = const.tile([P, P], BF16, name="ones")
        nc.vector.memset(ones[:], 1.0)
        warm = const.tile([P, 1], F32, name="warm")
        nc.vector.memset(warm[:], 0.0)
        nc.scalar.activation(out=warm[:], in_=warm[:], func=ACT.Sigmoid)
        twos = const.tile([P, 2, BATCH_TILES], F32, name="twos")
        nc.vector.memset(twos[:], 2.0)
        rate = const.tile([P, 32], F32, name="rate")
        td = const.tile([P, 2, 16], BF16, name="td")
        decay = const.tile([P, 2, BATCH_TILES], F32, name="decay")

        def load_bias(gates, first):
            row = bias_tiles[gates]
            nc.sync.dma_start(
                out=row[0:1, 0 : OUT * len(gates)],
                in_=b_hh[first : first + OUT * len(gates)].rearrange("(o c) -> o c", o=1),
            )

        def load_decay():
            row = bias_tiles["g"]
            nc.sync.dma_start(out=row[0:1, OUT + 16 : OUT + 17], in_=b.rearrange("(o c) -> o c", o=1))
            nc.sync.dma_start(out=row[0:1, OUT + 32 : OUT + 33], in_=a.rearrange("(o c) -> o c", o=1))
            nc.sync.dma_start(out=td[:, 0, 0:BATCH_TILES], in_=td0.rearrange("(p t) -> p t", p=P))
            nc.sync.dma_start(out=td[:, 1, 0:BATCH_TILES], in_=td1.rearrange("(p t) -> p t", p=P))

        raws = {}

        def load_activations(key, source, pool, pieces):
            raw = pool.tile([P, ROW_TILES, K], BF16, name="raw" if pool is raw_pool else key + "_raw")
            rows = source.rearrange("(p j) k -> p j k", p=P)
            step = ROW_TILES // pieces
            for j in range(0, ROW_TILES, step):
                nc.sync.dma_start(out=raw[:, j : j + step, :], in_=rows[:, j : j + step, :])
            raws[key] = raw

        def load_weights(gate, number, parts=range(2)):
            if (gate, number) not in raws:
                raws[gate, number] = raw_pool.tile([P, ROW_TILES, K], BF16, name="raw")
            raw = raws[gate, number]
            if gate == "g":
                pieces = [(w_hh, 2 * OUT + (2 * number + n) * QUARTER) for n in range(2)]
            else:
                peephole = w_pi if gate == "i" else w_pf
                pieces = [
                    (w_hh, GATE_COLUMN[gate] + number * QUARTER),
                    (peephole, number * QUARTER),
                ]
            for n in parts:
                source, first = pieces[n]
                nc.sync.dma_start(
                    out=raw[:, 2 * n : 2 * n + 2, :],
                    in_=source[first : first + QUARTER, :].rearrange("(p j) k -> p j k", p=P),
                )

        xg_parts = {}

        def load_xg(gate, half):
            first = GATE_COLUMN[gate] + half * 2 * QUARTER
            part = gate_pool.tile([P, BATCH_TILES, 2 * QUARTER], BF16, name="xg_%s%d" % (gate, half))
            nc.sync.dma_start(
                out=part[:],
                in_=xg[:, first : first + 2 * QUARTER].rearrange("(p t) c -> p t c", p=P),
            )
            xg_parts[gate, half] = part

        load_activations("hx", hx, raw_pool, 2)
        load_bias("g", 2 * OUT)
        load_weights("g", 0, (0,))
        load_xg("g", 0)
        load_weights("g", 0, (1,))
        load_bias("if", 0)
        load_decay()
        load_xg("g", 1)
        load_weights("g", 1)
        load_xg("f", 0)
        load_activations("cx", cx, const, 1)
        load_weights("f", 0)
        load_xg("i", 0)
        load_weights("i", 0)
        load_xg("f", 1)
        load_weights("f", 1)
        load_xg("i", 1)
        load_weights("i", 1)
        load_weights("f", 2)
        load_weights("i", 2)
        load_weights("f", 3)
        load_weights("i", 3)

        flipped = {}
        grouped = {}
        quantised = {}
        spreads = {}
        pre = {}
        accs = {}

        def transpose_block(key, tiles=range(ROW_TILES)):
            words = raws[key][:].rearrange("p j k -> p (j k)").bitcast(F32)
            for j in tiles:
                bank = flip_psum.tile([P, 2 * PASSES, P], F32, name="flipped", tag="flip")
                for q in range(2 * PASSES):
                    first = j * WORDS + q * P
                    nc.tensor.transpose(bank[:, q, :], words[:, first : first + P], ident[:])
                flipped[key, j] = bank

        def group_block(key):
            tile = grouped_pool.tile([P, PASSES * BLOCK * 4], BF16, name="grouped", align_bytes=256)
            target = tile[:].bitcast(F32).rearrange("p (g r u) -> p g r u", g=PASSES, u=2)
            for j in range(ROW_TILES):
                nc.scalar.copy(
                    out=target[:, :, j * P : (j + 1) * P, :],
                    in_=flipped[key, j][:].rearrange("p (g u) r -> p g r u", u=2),
                )
            grouped[key] = tile

        def quantise_block(key):
            pool, name = (const, key) if key in ("hx", "cx") else (weight_pool, "w")
            codes = pool.tile([P, PASSES, BLOCK], U32, name=name + "_codes", align_bytes=256)
            scales = pool.tile([P, PASSES, BLOCK], U8, name=name + "_scales", align_bytes=256)
            nc.vector.quantize_mx(
                out=codes[:].rearrange("p g r -> p (g r)").bitcast(FP8X4),
                scales=scales[:].rearrange("p g r -> p (g r)"),
                in_=grouped[key][:],
            )
            quantised[key] = (codes, scales)

        def spread_bias(gate, half, pool, tag):
            bank = pool.tile([P, 2 * QUARTER], F32, name="spread", tag=tag)
            nc.tensor.matmul(
                out=bank[:],
                lhsT=ones[:],
                rhs=bias_rows[gate][:, half * 2 * QUARTER : (half + 1) * 2 * QUARTER],
                start=True,
                stop=True,
            )
            spreads[gate, half] = bank

        def keep_bias(gate, half):
            spread_bias(gate, half, flip_psum, "flip")
            kept = const.tile([P, 2 * QUARTER], BF16, name="bias_%s%d" % (gate, half))
            nc.scalar.copy(out=kept[:], in_=spreads[gate, half][:])
            spreads[gate, half] = kept

        def new_pre(gate, number):
            if (gate, number) not in pre:
                pre[gate, number] = gate_pool.tile(
                    [P, BATCH_TILES, QUARTER], F32, name="pre_%s%d" % (gate, number)
                )

        def add_bias(engine, gate, number, pairs=None):
            if (gate, number) not in pre:
                pre[gate, number] = gate_pool.tile(
                    [P, BATCH_TILES, QUARTER], F32, name="pre_%s%d" % (gate, number)
                )
            half, odd = divmod(number, 2)
            cols = slice(odd * QUARTER, (odd + 1) * QUARTER)
            step = BATCH_TILES if pairs is None else 2
            for t in range(0, BATCH_TILES, step) if pairs is None else [2 * pair for pair in pairs]:
                rows = slice(t, t + step)
                engine.tensor_tensor(
                    out=pre[gate, number][:, rows, :],
                    in0=xg_parts[gate, half][:, rows, cols],
                    in1=spreads[gate, half][:, cols].unsqueeze(1).to_broadcast([P, step, QUARTER]),
                    op=ALU.add,
                )

        def multiply(gate, number, pairs=range(2)):
            codes, scales = quantised[gate, number]
            if gate == "g":
                units = [(2 * number + n, [("hx", n)]) for n in range(2)]
            else:
                units = [(number, [("hx", 0), ("cx", 1)])]
            for unit, operands in units:
                passes = [(source, n, g) for source, n in operands for g in range(PASSES)]
                for pair in pairs:
                    bank = acc_psum.tile([P, 2, QUARTER], F32, name="acc", tag="acc")
                    accs[gate, unit, pair] = bank
                    for slot in range(2):
                        t = 2 * pair + slot
                        batch = slice(t * P, (t + 1) * P)
                        for position, (source, n, g) in enumerate(passes):
                            act_codes, act_scales = quantised[source]
                            cols = slice(n * QUARTER, (n + 1) * QUARTER)
                            nc.tensor.matmul_mx(
                                out=bank[:, slot, :],
                                lhsT=act_codes[:, g, batch].bitcast(FP8X4),
                                lhsT_scale=act_scales[:, g, batch],
                                rhs=codes[:, g, cols].bitcast(FP8X4),
                                rhs_scale=scales[:, g, cols],
                                start=(position == 0),
                                stop=(position == len(passes) - 1),
                            )

        def activate(gate, number, pairs=range(2)):
            for pair in pairs:
                part = pre[gate, number][:, 2 * pair : 2 * pair + 2, :]
                nc.scalar.activation(
                    out=part, in_=part, func=ACT.Tanh if gate == "g" else ACT.Sigmoid
                )

        def finish_gate(gate, number, pairs):
            tile = pre[gate, number]
            for pair in pairs:
                part = tile[:, 2 * pair : 2 * pair + 2, :]
                by_row = part.rearrange("b t (p j) -> b t p j", j=2)
                nc.vector.tensor_tensor(
                    out=by_row,
                    in0=accs[gate, number, pair][:].rearrange("b t (j p) -> b t p j", j=2),
                    in1=by_row,
                    op=ALU.add,
                )

        def scale_gate(gate, number, tiles):
            tile = pre[gate, number]
            for t in tiles:
                if gate == "f":
                    row, other = 0, raws["cx"][:, t, number * QUARTER : (number + 1) * QUARTER]
                else:
                    row, other = 1, pre["g", number][:, t, :]
                nc.vector.scalar_tensor_tensor(
                    out=tile[:, t, :], in0=tile[:, t, :], scalar=decay[:, row, t : t + 1],
                    in1=other, op0=ALU.mult, op1=ALU.mult,
                )

        out_rows = out.rearrange("(p t) c -> p t c", p=P)

        def add_and_store(engine, number, pairs):
            for pair in pairs:
                rows = slice(2 * pair, 2 * pair + 2)
                part = pre["i", number][:, rows, :]
                engine.tensor_tensor(
                    out=part, in0=part, in1=pre["f", number][:, rows, :], op=ALU.add
                )
                nc.sync.dma_start(
                    out=out_rows[:, rows, number * QUARTER : (number + 1) * QUARTER], in_=part
                )

        def sum_by_matmul(number, pairs):
            for pair in pairs:
                rows = slice(2 * pair, 2 * pair + 2)
                part = pre["i", number][:, rows, :]
                bank = acc_psum.tile([P, 2, QUARTER], F32, name="total", tag="acc")
                for term, last in ((part, False), (pre["f", number][:, rows, :], True)):
                    nc.tensor.matmul(
                        out=bank[:].rearrange("b t c -> b (t c)"), lhsT=ident[:],
                        rhs=term.rearrange("b t c -> b (t c)"), start=not last, stop=last,
                    )
                nc.scalar.copy(out=part, in_=bank[:])
                nc.sync.dma_start(
                    out=out_rows[:, rows, number * QUARTER : (number + 1) * QUARTER], in_=part
                )

        def make_decay():
            bank = flip_psum.tile([P, 2 * QUARTER], F32, name="rates", tag="flip")
            nc.tensor.matmul(
                out=bank[:, 0:32], lhsT=ones[:], rhs=bias_tiles["g"][:, OUT + 16 : OUT + 48],
                start=True, stop=True,
            )
            nc.vector.tensor_copy(out=rate[:], in_=bank[:, 0:32])
            exponent = const.tile([P, 2, BATCH_TILES], F32, name="exponent")
            nc.vector.tensor_scalar(
                out=exponent[:], in0=td[:, :, 0:BATCH_TILES], scalar1=rate[:, 0:1], scalar2=-LOG2_E,
                op0=ALU.mult, op1=ALU.mult,
            )
            nc.gpsimd.tensor_tensor(out=decay[:], in0=twos[:], in1=exponent[:], op=ALU.pow)

        transpose_block("hx")
        group_block("hx")
        spread_bias("g", 0, acc_psum, "acc")
        add_bias(nc.vector, "g", 0)
        quantise_block("hx")
        add_bias(nc.vector, "g", 1)
        transpose_block(("g", 0))
        spread_bias("g", 1, acc_psum, "acc")
        group_block(("g", 0))
        make_decay()
        quantise_block(("g", 0))
        keep_bias("f", 0)
        keep_bias("i", 0)
        keep_bias("f", 1)
        keep_bias("i", 1)

        transpose_block(("g", 1))
        group_block(("g", 1))
        add_bias(nc.vector, "g", 2)
        add_bias(nc.vector, "g", 3)
        multiply("g", 0)
        quantise_block(("g", 1))
        nc.vector.tensor_scalar_mul(out=decay[:], in0=decay[:], scalar1=rate[:, 16:17])
        add_bias(nc.vector, "f", 0)

        transpose_block("cx")
        group_block("cx")
        transpose_block(("f", 0))
        group_block(("f", 0))
        finish_gate("g", 0, range(2))
        activate("g", 0)
        finish_gate("g", 1, range(2))
        activate("g", 1)
        multiply("g", 1)
        quantise_block("cx")
        add_bias(nc.gpsimd, "f", 1, (0, 1))
        quantise_block(("f", 0))

        transpose_block(("i", 0))
        group_block(("i", 0))
        finish_gate("g", 2, range(2))
        activate("g", 2)
        finish_gate("g", 3, range(2))
        activate("g", 3)

        multiply("f", 0)
        add_bias(nc.vector, "i", 0)
        quantise_block(("i", 0))
        add_bias(nc.gpsimd, "i", 1, (0, 1))
        transpose_block(("f", 1))
        group_block(("f", 1))
        add_bias(nc.vector, "f", 2)
        finish_gate("f", 0, range(2))
        activate("f", 0)

        multiply("i", 0)
        quantise_block(("f", 1))
        transpose_block(("i", 1))
        group_block(("i", 1))
        add_bias(nc.gpsimd, "f", 3, (0, 1))
        scale_gate("f", 0, range(4))
        finish_gate("i", 0, range(2))
        activate("i", 0)

        multiply("f", 1)
        quantise_block(("i", 1))
        transpose_block(("f", 2))
        group_block(("f", 2))
        add_bias(nc.vector, "i", 2)
        scale_gate("i", 0, range(4))
        finish_gate("f", 1, range(2))
        activate("f", 1)

        multiply("i", 1)
        quantise_block(("f", 2))
        transpose_block(("i", 2))
        group_block(("i", 2))
        add_bias(nc.gpsimd, "i", 3, (0, 1))
        scale_gate("f", 1, range(4))
        finish_gate("i", 1, range(2))
        activate("i", 1)

        multiply("f", 2)
        quantise_block(("i", 2))
        transpose_block(("f", 3))
        group_block(("f", 3))
        add_and_store(nc.gpsimd, 0, range(2))
        scale_gate("i", 1, range(4))
        finish_gate("f", 2, range(2))
        activate("f", 2)

        multiply("i", 2, (0,))
        transpose_block(("i", 3), (0, 1))
        multiply("i", 2, (1,))
        quantise_block(("f", 3))
        transpose_block(("i", 3), (2, 3))
        group_block(("i", 3))
        add_and_store(nc.gpsimd, 1, range(2))
        scale_gate("f", 2, range(4))
        finish_gate("i", 2, range(2))
        activate("i", 2)

        multiply("f", 3)
        quantise_block(("i", 3))
        scale_gate("i", 2, range(4))
        add_and_store(nc.gpsimd, 2, (1,))

        multiply("i", 3)
        finish_gate("f", 3, range(2))
        activate("f", 3)
        finish_gate("i", 3, range(2))
        activate("i", 3)
        sum_by_matmul(2, (0,))
        scale_gate("f", 3, range(4))
        scale_gate("i", 3, (0, 1,))
        scale_gate("i", 3, (2, 3,))
        add_and_store(nc.vector, 3, (0,))
        add_and_store(nc.vector, 3, (1,))
